import numpy as np
import ml_dtypes


def mxq(x, axis, fmt="e4m3"):
    dtype, down = {"e4m3": (ml_dtypes.float8_e4m3fn, 7), "e5m2": (ml_dtypes.float8_e5m2, 14)}[fmt]
    v = np.moveaxis(np.asarray(x, np.float32).astype(ml_dtypes.bfloat16).astype(np.float64), axis, -1)
    blocks = v.reshape(v.shape[:-1] + (-1, 32))
    amax = np.abs(blocks).max(-1, keepdims=True)
    byte = np.maximum(np.where(amax > 0, np.frexp(amax)[1] - 1 + 127, 0) - down, 1)
    scale = np.exp2(byte - 127.0)
    codes = (blocks / scale).astype(np.float32).astype(dtype).astype(np.float64)
    return np.moveaxis((codes * scale).reshape(v.shape), -1, axis)


WIDE = False


def mx_kscale(k):
    if not WIDE:
        return np.ones(k)
    levels = np.array([10, -10, 5, -5, 0])
    a = np.random.permutation(np.resize(levels, k // 512 * 4)).reshape(k // 512, 4)
    idx = np.arange(k)
    return np.exp2(a[idx // 512, idx % 128 // 32])


BF16 = ml_dtypes.bfloat16


def bf(x):
    return np.asarray(x, np.float32).astype(BF16)


def f64(x):
    return np.asarray(x).astype(np.float64)


B, F_IN, H, D, N = 6144, 768, 1024, 512, 256
C = 3.0
SQRT_C = np.sqrt(C)
MIN_NORM = 1e-15
EPS = 1e-5
TEMP = 0.07


def artanh(v):
    return 0.5 * np.log((1.0 + v) / (1.0 - v))


def expmap0(u):
    un = np.maximum(np.sqrt((u * u).sum(-1, keepdims=True)), MIN_NORM)
    return np.tanh(SQRT_C * un) * u / (SQRT_C * un)


def profile():
    d = 1.0 / np.sqrt(1.0 + np.arange(D))
    return d / np.sqrt((d * d).sum())


def setup_inputs():
    s = mx_kscale(H)
    d = profile()
    g = np.random.standard_normal((N, D)) * d
    return {"h_mlp": bf(np.random.standard_normal((B, H)) * 0.65 * s),
            "W3": bf(np.random.standard_normal((H, D)) * 0.8 / np.sqrt(H) * d / s[:, None]),
            "b3": bf(np.random.standard_normal(D) * 0.2 * d),
            "prototypes": bf(g / np.sqrt((g * g).sum(1, keepdims=True)) * 0.95 / C)}


def reference(h_mlp, W3, b3, prototypes):
    p = f64(prototypes)
    u = (mxq(f64(h_mlp), 1, "e4m3") @ mxq(f64(W3), 0, "e4m3")) + f64(b3)
    hyp = expmap0(u)
    A = (p * p).sum(-1)
    Bn = (hyp * hyp).sum(-1)
    P = mxq(hyp, 1, "e4m3") @ mxq(p, 1, "e4m3").T
    alpha = 1.0 - 2.0 * C * P + C * Bn[:, None]
    beta = 1.0 - C * A[None, :]
    denom = np.maximum(1.0 - 2.0 * C * P + (C * C) * A[None, :] * Bn[:, None], MIN_NORM)
    num_sq = alpha * alpha * A[None, :] + beta * beta * Bn[:, None] - 2.0 * alpha * beta * P
    mnorm = np.sqrt(np.maximum(num_sq, MIN_NORM)) / denom
    arg = np.minimum(SQRT_C * mnorm, 1.0 - EPS)
    dist = (2.0 / SQRT_C) * artanh(arg)
    return -dist / TEMP, hyp

@@ -1,0 +1,439 @@
+import math
+from contextlib import ExitStack
+
+import concourse.mybir as mybir
+from concourse.masks import make_identity
+
+F32 = mybir.dt.float32
+BF16 = mybir.dt.bfloat16
+U32 = mybir.dt.uint32
+U8 = mybir.dt.uint8
+FP8X4 = mybir.dt.float8_e4m3fn_x4
+ALU = mybir.AluOpType
+ACT = mybir.ActivationFunctionType
+
+B, H, D, N = 6144, 1024, 512, 256
+FLOPS = 2 * B * H * D + 2 * B * D * N
+
+P = 128
+NT = B // P
+NQ = NT // 4
+NJ = NT // 2
+C = 3.0
+SQRT_C = math.sqrt(C)
+KLOG = 1.0 / (0.07 * SQRT_C)
+LOG_RMAX = math.log((2.0 - 1e-5) / 1e-5)
+ZMIN = SQRT_C * 1e-15
+GAMMA_MIN = 1e-10
+
+LQ = 2
+CYCLES = (9, 3)
+CD_DELAY = 2
+CD_CAP = 2.0
+C1_V = ()
+P3V_Q = ()
+P6_V = tuple(range(25, 48, 4))
+P4_G = ()
+O5_G = ()
+VARB = (10, 11)
+R1_BUFS = 6
+
+
+def tile_hyperbolicuniform_pa_t_kernel(tc, h_mlp, W3, b3, prototypes, out_0, out_1):
+    nc = tc.nc
+    h_v = h_mlp.rearrange("(p n) k -> p n k", n=NT)
+    hyp_v = out_1.rearrange("(p n) d -> p n d", n=NT)
+    log_v = out_0.rearrange("(p n) j -> p n j", n=NT)
+
+    with ExitStack() as ctx:
+        ctx.enter_context(tc.manual_schedule())
+        const = ctx.enter_context(tc.tile_pool(name="const", bufs=1))
+        hpool = ctx.enter_context(tc.tile_pool(name="hpool", bufs=4))
+        ubpool = ctx.enter_context(tc.tile_pool(name="ubpool", bufs=NQ))
+        grp = ctx.enter_context(tc.tile_pool(name="grp", bufs=4))
+        cod = ctx.enter_context(tc.tile_pool(name="cod", bufs=4))
+        r1pool = ctx.enter_context(tc.tile_pool(name="r1pool", bufs=R1_BUFS))
+        epool = ctx.enter_context(tc.tile_pool(name="epool", bufs=4))
+        tp = ctx.enter_context(tc.psum_pool(name="tp", bufs=4))
+        mm = ctx.enter_context(tc.psum_pool(name="mm", bufs=4))
+
+        ident = const.tile([P, P], F32, name="ident")
+        ident_bf = const.tile([P, P], BF16, name="ident_bf")
+        half = const.tile([P, 4], F32, name="half")
+        make_identity(nc, ident_bf[:])
+        make_identity(nc, ident[:])
+        nc.gpsimd.memset(half[:], 0.5)
+
+        bias_bc = const.tile([P, D], BF16, name="bias_bc")
+        pr = const.tile([P, 2, D], BF16, name="pr")
+        nc.scalar.dma_start(out=pr[:], in_=prototypes.rearrange("(c p) d -> p c d", c=2))
+        nc.scalar.dma_start(out=bias_bc[:], in_=b3.partition_broadcast(P))
+
+        h_tiles = {}
+
+        def load_h(k, parts=1):
+            ht = hpool.tile([P, 4, H], BF16, name="h_sb", tag="h_sb")
+            h_tiles[k] = ht
+            step = 4 // parts
+            for a in range(0, 4, step):
+                nc.sync.dma_start(out=ht[:, a : a + step, :], in_=h_v[:, 4 * k + a : 4 * k + a + step, :])
+
+        w_raw = const.tile([P, 2, 2, 2, D], BF16, name="w_raw")
+        wg = const.tile([P, 2, D, 4], BF16, name="wg", align_bytes=64)
+        wc = const.tile([P, 2, D], U32, name="wc", align_bytes=64)
+        ws = const.tile([P, 2, D], U8, name="ws", align_bytes=64)
+
+        for g in range(2):
+            nc.sync.dma_start(
+                out=w_raw[:, g],
+                in_=W3[512 * g : 512 * (g + 1), :].rearrange("(u p e) d -> p u e d", u=2, e=2),
+            )
+        load_h(0, parts=2)
+        for k in range(1, 4):
+            load_h(k)
+
+        def regroup_w(g):
+            nc.vector.tensor_copy(
+                out=wg[:, g].rearrange("p (c i) t -> p c t i", i=4),
+                in_=w_raw[:, g].rearrange("p u e (c i) -> p c (u e) i", i=4),
+            )
+
+        def quantise_w(g):
+            nc.vector.quantize_mx(
+                out=wc[:, g, :].bitcast(FP8X4),
+                scales=ws[:, g, :],
+                in_=wg[:, g].rearrange("p d t -> p (d t)"),
+            )
+
+        zz = const.tile([P, NT], F32, name="zz")
+        zzv = const.tile([P, NT], F32, name="zzv")
+        zt = const.tile([P, NT], F32, name="zt")
+        th = const.tile([P, NT], F32, name="th")
+        zc = const.tile([P, NT], F32, name="zc")
+        rz = const.tile([P, NT], F32, name="rz")
+        fs = const.tile([P, NT], F32, name="fs")
+        cb = const.tile([P, NT], F32, name="cb")
+        hb = const.tile([P, NT], F32, name="hb")
+        gm = const.tile([P, NT], F32, name="gm")
+        gc = const.tile([P, NT], F32, name="gc")
+        ig = const.tile([P, NT], F32, name="ig")
+        sv = const.tile([P, NT], F32, name="sv")
+        junk = const.tile([P, D], BF16, name="junk")
+        junkv = const.tile([P, D], BF16, name="junkv")
+
+        a2 = const.tile([P, 2], F32, name="a2")
+        bt = const.tile([P, 2], F32, name="bt")
+        hv = const.tile([P, 4], F32, name="hv")
+        pg = const.tile([P, N, 4], BF16, name="pg", align_bytes=64)
+        pc = const.tile([P, N], U32, name="pc", align_bytes=64)
+        psc = const.tile([P, N], U8, name="psc", align_bytes=64)
+        haib = const.tile([P, 2, N], F32, name="haib")
+        proto_ps = {}
+
+        for c in range(2):
+            nc.scalar.activation(out=junk[:], in_=pr[:, c, :], func=ACT.Square, accum_out=a2[:, c : c + 1])
+        for c in range(2):
+            ps = mm.tile([P, 4, P], BF16, name="tpp", tag="mm")
+            proto_ps[c] = ps
+            for t in range(4):
+                nc.tensor.transpose(ps[:, t, :], pr[:, c, P * t : P * (t + 1)], ident_bf[:])
+        regroup_w(0)
+        nc.vector.tensor_scalar(out=hv[:, 0:2], in0=a2[:], scalar1=0.5, scalar2=None, op0=ALU.mult)
+        nc.vector.tensor_scalar(out=bt[:], in0=a2[:], scalar1=-C, scalar2=1.0, op0=ALU.mult, op1=ALU.add)
+        regroup_w(1)
+        nc.vector.reciprocal(out=hv[:, 2:4], in_=bt[:])
+        quantise_w(0)
+        psb = mm.tile([P, 4, P], F32, name="tpb", tag="mm")
+        for m in range(4):
+            nc.tensor.matmul(
+                out=psb[:, m, :], lhsT=hv[:, m : m + 1].to_broadcast([P, P]), rhs=ident[:], start=True, stop=True
+            )
+        for c in range(2):
+            nc.scalar.copy(out=pg[:, P * c : P * (c + 1), :], in_=proto_ps[c][:].rearrange("p t j -> p j t"))
+        nc.scalar.copy(out=haib[:].rearrange("p v j -> p (v j)"), in_=psb[:].rearrange("p m j -> p (m j)"))
+        quantise_w(1)
+        nc.vector.quantize_mx(out=pc[:].bitcast(FP8X4), scales=psc[:], in_=pg[:].rearrange("p j t -> p (j t)"))
+
+        ub_tiles = {}
+        q_tiles = {}
+        tp_tiles = {}
+        grp_tiles = {}
+        cod_tiles = {}
+        mm_tiles = {}
+        r1_tiles = {}
+
+        def stage_transpose(J):
+            for i in range(2):
+                t = 2 * J + i
+                ps = tp.tile([P, 4, P], F32, name="tps", tag="tp")
+                tp_tiles[t] = ps
+                if J < NJ:
+                    src = h_tiles[t // 4][:].bitcast(F32)[:, t % 4, :]
+                else:
+                    src = ub_tiles[(t - NT) // 4][:, (t - NT) % 4, :]
+                for c in range(4):
+                    nc.tensor.transpose(ps[:, c, :], src[:, P * c : P * (c + 1)], ident[:])
+            if J < NJ and J % 2 == 1 and J // 2 + 4 < NQ:
+                load_h(J // 2 + 4)
+
+        def stage_copy(J):
+            if J < NJ:
+                g = grp.tile([P, 2, 2, P, 4], BF16, name="hgrp", tag="grp", align_bytes=64)
+                g32 = g[:].bitcast(F32)
+                for i in range(2):
+                    t = 2 * J + i
+                    src = tp_tiles[t][:].rearrange("p (g u) b -> p g b u", u=2)
+                    if t in C1_V:
+                        nc.vector.tensor_copy(out=g32[:, i], in_=src)
+                    else:
+                        nc.scalar.copy(out=g32[:, i], in_=src)
+            else:
+                g = grp.tile([P, 2, P, 4], BF16, name="ygrp", tag="grp", align_bytes=64)
+                for i in range(2):
+                    t = 2 * J + i
+                    src = tp_tiles[t][:].rearrange("p t b -> p b t")
+                    if (t - NT) in P6_V:
+                        nc.vector.tensor_copy(out=g[:, i], in_=src)
+                    else:
+                        nc.scalar.copy(out=g[:, i], in_=src)
+            grp_tiles[J] = g
+
+        def stage_quantise(J):
+            width = 512 if J < NJ else 256
+            c = cod.tile([P, width], U32, name="codes", tag="codes", align_bytes=64)
+            s_ = cod.tile([P, width], U8, name="scales", tag="scales", align_bytes=64)
+            cod_tiles[J] = (c, s_)
+            g = grp_tiles[J]
+            flat = g[:].rearrange("p i g b t -> p (i g b t)") if J < NJ else g[:].rearrange("p i b t -> p (i b t)")
+            nc.vector.quantize_mx(out=c[:].bitcast(FP8X4), scales=s_[:], in_=flat)
+
+        def stage_mx(J):
+            c, s_ = cod_tiles[J]
+            if J < NJ:
+                for i in range(2):
+                    acc = mm.tile([P, D], F32, name="acc", tag="mm")
+                    mm_tiles[2 * J + i] = acc
+                    for g in range(2):
+                        cols = slice(256 * i + P * g, 256 * i + P * (g + 1))
+                        nc.tensor.matmul_mx(
+                            out=acc[:],
+                            lhsT=c[:, cols].bitcast(FP8X4),
+                            lhsT_scale=s_[:, cols],
+                            rhs=wc[:, g, :].bitcast(FP8X4),
+                            rhs_scale=ws[:, g, :],
+                            start=(g == 0),
+                            stop=(g == 1),
+                        )
+            else:
+                acc = mm.tile([P, 2, N], F32, name="accx", tag="mm")
+                mm_tiles[2 * J] = acc
+                for i in range(2):
+                    cols = slice(P * i, P * (i + 1))
+                    nc.tensor.matmul_mx(
+                        out=acc[:, i, :],
+                        lhsT=c[:, cols].bitcast(FP8X4),
+                        lhsT_scale=s_[:, cols],
+                        rhs=pc[:].bitcast(FP8X4),
+                        rhs_scale=psc[:],
+                        start=True,
+                        stop=True,
+                    )
+
+        def stage_evacuate(J):
+            if J < NJ:
+                for i in range(2):
+                    t = 2 * J + i
+                    if t % 4 == 0:
+                        ub_tiles[t // 4] = ubpool.tile([P, 4, D], F32, name="ub", tag="ub")
+                    nc.vector.tensor_tensor(
+                        out=ub_tiles[t // 4][:, t % 4, :], in0=mm_tiles[t][:], in1=bias_bc[:], op=ALU.add
+                    )
+            else:
+                es = []
+                for i in range(2):
+                    t = 2 * (J - NJ) + i
+                    e = epool.tile([P, N], F32, name="e", tag="e")
+                    es.append(e)
+                    nc.vector.scalar_tensor_tensor(
+                        out=e[:], in0=mm_tiles[2 * J][:, i, :], scalar=hb[:, t : t + 1], in1=haib[:, 0, :],
+                        op0=ALU.subtract, op1=ALU.subtract,
+                    )
+                for i in range(2):
+                    t = 2 * (J - NJ) + i
+                    if t % 4 == 0:
+                        q_tiles[t // 4] = ubpool.tile([P, 4, N], F32, name="q", tag="ub")
+                    nc.vector.scalar_tensor_tensor(
+                        out=q_tiles[t // 4][:, t % 4, :], in0=es[i][:], scalar=sv[:, t : t + 1], in1=haib[:, 1, :],
+                        op0=ALU.mult, op1=ALU.mult,
+                    )
+
+        def stage_norm(j):
+            for t in (2 * j, 2 * j + 1):
+                u = ub_tiles[t // 4][:, t % 4, :]
+                if t // 4 in P3V_Q:
+                    nc.vector.scalar_tensor_tensor(
+                        out=junkv[:], in0=u, scalar=C, in1=u, op0=ALU.mult, op1=ALU.mult, accum_out=zzv[:, t : t + 1]
+                    )
+                else:
+                    nc.scalar.activation(out=junk[:], in_=u, func=ACT.Square, scale=SQRT_C, accum_out=zz[:, t : t + 1])
+
+        def stage_pow(k):
+            cols = slice(4 * k, 4 * k + 4)
+            src = zzv if k in P3V_Q else zz
+            nc.gpsimd.tensor_tensor(out=zt[:, cols], in0=src[:, cols], in1=half[:], op=ALU.pow)
+
+        def stage_tanh(k):
+            cols = slice(4 * k, 4 * k + 4)
+            nc.scalar.activation(out=th[:, cols], in_=zt[:, cols], func=ACT.Tanh)
+            nc.vector.tensor_scalar(out=zc[:, cols], in0=zt[:, cols], scalar1=ZMIN, scalar2=None, op0=ALU.max)
+            nc.vector.reciprocal(out=rz[:, cols], in_=zc[:, cols])
+
+        def stage_factor(k):
+            cols = slice(4 * k, 4 * k + 4)
+            nc.vector.tensor_tensor(out=fs[:, cols], in0=th[:, cols], in1=rz[:, cols], op=ALU.mult)
+
+        def stage_scale(k, part):
+            for t in (4 * k + 2 * part, 4 * k + 2 * part + 1):
+                u = ub_tiles[k][:, t % 4, :]
+                if t in P4_G:
+                    nc.gpsimd.tensor_scalar(out=u, in0=u, scalar1=fs[:, t : t + 1], scalar2=0.0, op0=ALU.mult, op1=ALU.add)
+                else:
+                    nc.vector.tensor_scalar(out=u, in0=u, scalar1=fs[:, t : t + 1], scalar2=None, op0=ALU.mult)
+            if part == 1:
+                nc.sync.dma_start(out=hyp_v[:, 4 * k : 4 * k + 4, :], in_=ub_tiles[k][:])
+
+        def stage_rowconst(part):
+            cols = slice(24 * part, 24 * (part + 1))
+            nc.vector.tensor_tensor(out=cb[:, cols], in0=th[:, cols], in1=th[:, cols], op=ALU.mult)
+            nc.vector.tensor_scalar(out=gm[:, cols], in0=cb[:, cols], scalar1=-1.0, scalar2=1.0, op0=ALU.mult, op1=ALU.add)
+            nc.vector.tensor_scalar(out=hb[:, cols], in0=cb[:, cols], scalar1=0.5 / C, scalar2=None, op0=ALU.mult)
+            nc.vector.tensor_scalar(out=gc[:, cols], in0=gm[:, cols], scalar1=GAMMA_MIN, scalar2=None, op0=ALU.max)
+            nc.vector.reciprocal(out=ig[:, cols], in_=gc[:, cols])
+            nc.vector.tensor_scalar(out=sv[:, cols], in0=ig[:, cols], scalar1=-2.0 * C, scalar2=None, op0=ALU.mult)
+
+        def flat_q(k):
+            return q_tiles[k][:].rearrange("p i j -> p (i j)")
+
+        def stage_pre(k):
+            r1 = r1pool.tile([P, 4 * N], F32, name="r1", tag="r1")
+            r1_tiles[k] = r1
+            nc.vector.scalar_tensor_tensor(
+                out=r1[:], in0=flat_q(k), scalar=1.0, in1=flat_q(k), op0=ALU.add, op1=ALU.mult
+            )
+
+        def stage_sqrt(k):
+            if k in VARB:
+                nc.scalar.activation(out=r1_tiles[k][:], in_=r1_tiles[k][:], func=ACT.Sqrt)
+            else:
+                r1 = r1pool.tile([P, 4 * N], F32, name="r1", tag="r1")
+                r1_tiles[k] = r1
+                nc.scalar.activation(out=r1[:], in_=flat_q(k), func=ACT.Sqrt, bias=1.0)
+                nc.scalar.activation(out=flat_q(k), in_=flat_q(k), func=ACT.Sqrt)
+
+        def stage_sum(k):
+            if k in VARB:
+                nc.vector.scalar_tensor_tensor(
+                    out=flat_q(k), in0=r1_tiles[k][:], scalar=0.0, in1=flat_q(k), op0=ALU.max, op1=ALU.add
+                )
+            elif k in O5_G:
+                nc.gpsimd.tensor_tensor(out=flat_q(k), in0=flat_q(k), in1=r1_tiles[k][:], op=ALU.add)
+            else:
+                nc.vector.scalar_tensor_tensor(
+                    out=flat_q(k), in0=flat_q(k), scalar=0.0, in1=r1_tiles[k][:], op0=ALU.max, op1=ALU.add
+                )
+
+        def stage_ln(k):
+            if k in VARB:
+                nc.scalar.activation(out=flat_q(k), in_=flat_q(k), func=ACT.Ln, scale=2.0, bias=1.0)
+            else:
+                nc.scalar.activation(out=flat_q(k), in_=flat_q(k), func=ACT.Ln)
+
+        def stage_out(k):
+            nc.vector.tensor_scalar(
+                out=flat_q(k), in0=flat_q(k), scalar1=(-KLOG if k in VARB else -2.0 * KLOG), scalar2=-KLOG * LOG_RMAX,
+                op0=ALU.mult, op1=ALU.max,
+            )
+            nc.sync.dma_start(out=log_v[:, 4 * k : 4 * k + 4, :], in_=q_tiles[k][:])
+
+        items = []
+        a = 0
+        for n in CYCLES:
+            items.extend([("sqrt", k, NJ + 2 * k + 1 + CD_DELAY) for k in range(a, a + n)])
+            items.extend([("ln", k, NJ + 2 * k + 2 + CD_DELAY) for k in range(a, a + n)])
+            a += n
+        pend = []
+        done = [0, 0]
+
+        def follow(keep):
+            while len(pend) - done[0] > keep:
+                kind, k = pend[done[0]]
+                done[0] += 1
+                if kind == "sqrt":
+                    stage_sum(k)
+                else:
+                    stage_out(k)
+
+        for J in range(LQ + 1):
+            stage_transpose(J)
+            if J < LQ:
+                stage_copy(J)
+                stage_quantise(J)
+
+        NS = 2 * NJ
+        s = 0
+        credit = 0.0
+        while s < NS or done[1] < len(items) or done[0] < len(pend):
+            if s < NS:
+                stage_mx(s)
+            if s + LQ + 1 < NS:
+                stage_transpose(s + LQ + 1)
+            if s + LQ < NS:
+                stage_copy(s + LQ)
+            if s < NS:
+                stage_evacuate(s)
+            if s + LQ < NS:
+                stage_quantise(s + LQ)
+            j = s - 1
+            if 0 <= j < NJ:
+                stage_norm(j)
+                if j % 2 == 1:
+                    stage_pow(j // 2)
+            j = s - 2
+            if 0 <= j < NJ and j % 2 == 1:
+                stage_tanh(j // 2)
+            j = s - 3
+            if 0 <= j < NJ and j % 2 == 1:
+                stage_factor(j // 2)
+                stage_scale(j // 2, 0)
+            j = s - 4
+            if 0 <= j < NJ and j % 2 == 1:
+                stage_scale(j // 2, 1)
+            k = (s - NJ - 2) // 2
+            if (s - NJ) % 2 == 0 and k in VARB:
+                stage_pre(k)
+            if s == 15:
+                stage_rowconst(0)
+            if s == 27:
+                stage_rowconst(1)
+            follow(1)
+            credit = credit + (CD_CAP if s < NS else 100.0)
+            while done[1] < len(items):
+                kind, k, first_step = items[done[1]]
+                cost = 2.0 if kind == "sqrt" and k not in VARB else 1.0
+                if first_step > s or credit < cost:
+                    break
+                done[1] += 1
+                credit -= cost
+                if kind == "sqrt":
+                    stage_sqrt(k)
+                else:
+                    if ("sqrt", k) in pend[done[0] :]:
+                        follow(0)
+                    stage_ln(k)
+                pend.append((kind, k))
+                if s >= NS:
+                    follow(1)
+            credit = min(credit, 2.0)
+            if s >= NS and done[1] == len(items):
+                follow(0)
+            s += 1

@@ -27,12 +27,13 @@ ZMIN = SQRT_C * 1e-15
 GAMMA_MIN = 1e-10
 
 LQ = 2
+LP3 = 2
 CYCLES = (9, 3)
 CD_DELAY = 2
 CD_CAP = 2.0
-C1_V = ()
+C1_V = (5, 7, 9, 11, 13, 15)
 P3V_Q = ()
-P6_V = tuple(range(25, 48, 4))
+P6_V = (33, 37, 41, 45)
 P4_G = ()
 O5_G = ()
 VARB = (10, 11)
@@ -54,6 +55,7 @@ def tile_hyperbolicuniform_pa_t_kernel(tc, h_mlp, W3, b3, prototypes, out_0, out
         cod = ctx.enter_context(tc.tile_pool(name="cod", bufs=4))
         r1pool = ctx.enter_context(tc.tile_pool(name="r1pool", bufs=R1_BUFS))
         epool = ctx.enter_context(tc.tile_pool(name="epool", bufs=4))
+        junkp = ctx.enter_context(tc.tile_pool(name="junkp", bufs=4))
         tp = ctx.enter_context(tc.psum_pool(name="tp", bufs=4))
         mm = ctx.enter_context(tc.psum_pool(name="mm", bufs=4))
 
@@ -119,7 +121,6 @@ def tile_hyperbolicuniform_pa_t_kernel(tc, h_mlp, W3, b3, prototypes, out_0, out
         ig = const.tile([P, NT], F32, name="ig")
         sv = const.tile([P, NT], F32, name="sv")
         junk = const.tile([P, D], BF16, name="junk")
-        junkv = const.tile([P, D], BF16, name="junkv")
 
         a2 = const.tile([P, 2], F32, name="a2")
         bt = const.tile([P, 2], F32, name="bt")
@@ -161,6 +162,7 @@ def tile_hyperbolicuniform_pa_t_kernel(tc, h_mlp, W3, b3, prototypes, out_0, out
         cod_tiles = {}
         mm_tiles = {}
         r1_tiles = {}
+        e_tiles = {}
 
         def stage_transpose(J):
             for i in range(2):
@@ -249,33 +251,36 @@ def tile_hyperbolicuniform_pa_t_kernel(tc, h_mlp, W3, b3, prototypes, out_0, out
                         out=ub_tiles[t // 4][:, t % 4, :], in0=mm_tiles[t][:], in1=bias_bc[:], op=ALU.add
                     )
             else:
-                es = []
                 for i in range(2):
                     t = 2 * (J - NJ) + i
                     e = epool.tile([P, N], F32, name="e", tag="e")
-                    es.append(e)
+                    e_tiles[t] = e
                     nc.vector.scalar_tensor_tensor(
                         out=e[:], in0=mm_tiles[2 * J][:, i, :], scalar=hb[:, t : t + 1], in1=haib[:, 0, :],
                         op0=ALU.subtract, op1=ALU.subtract,
                     )
-                for i in range(2):
-                    t = 2 * (J - NJ) + i
-                    if t % 4 == 0:
-                        q_tiles[t // 4] = ubpool.tile([P, 4, N], F32, name="q", tag="ub")
-                    nc.vector.scalar_tensor_tensor(
-                        out=q_tiles[t // 4][:, t % 4, :], in0=es[i][:], scalar=sv[:, t : t + 1], in1=haib[:, 1, :],
-                        op0=ALU.mult, op1=ALU.mult,
-                    )
+
+        def stage_q(J):
+            for i in range(2):
+                t = 2 * (J - NJ) + i
+                if t % 4 == 0:
+                    q_tiles[t // 4] = ubpool.tile([P, 4, N], F32, name="q", tag="ub")
+                nc.vector.scalar_tensor_tensor(
+                    out=q_tiles[t // 4][:, t % 4, :], in0=e_tiles[t][:], scalar=sv[:, t : t + 1], in1=haib[:, 1, :],
+                    op0=ALU.mult, op1=ALU.mult,
+                )
 
         def stage_norm(j):
             for t in (2 * j, 2 * j + 1):
                 u = ub_tiles[t // 4][:, t % 4, :]
                 if t // 4 in P3V_Q:
+                    jk = junkp.tile([P, D], BF16, name="junkv", tag="junkv")
                     nc.vector.scalar_tensor_tensor(
-                        out=junkv[:], in0=u, scalar=C, in1=u, op0=ALU.mult, op1=ALU.mult, accum_out=zzv[:, t : t + 1]
+                        out=jk[:], in0=u, scalar=C, in1=u, op0=ALU.mult, op1=ALU.mult, accum_out=zzv[:, t : t + 1]
                     )
                 else:
-                    nc.scalar.activation(out=junk[:], in_=u, func=ACT.Square, scale=SQRT_C, accum_out=zz[:, t : t + 1])
+                    jk = junkp.tile([P, D], BF16, name="junks", tag="junks")
+                    nc.scalar.activation(out=jk[:], in_=u, func=ACT.Square, scale=SQRT_C, accum_out=zz[:, t : t + 1])
 
         def stage_pow(k):
             cols = slice(4 * k, 4 * k + 4)
@@ -286,6 +291,9 @@ def tile_hyperbolicuniform_pa_t_kernel(tc, h_mlp, W3, b3, prototypes, out_0, out
             cols = slice(4 * k, 4 * k + 4)
             nc.scalar.activation(out=th[:, cols], in_=zt[:, cols], func=ACT.Tanh)
             nc.vector.tensor_scalar(out=zc[:, cols], in0=zt[:, cols], scalar1=ZMIN, scalar2=None, op0=ALU.max)
+
+        def stage_recip(k):
+            cols = slice(4 * k, 4 * k + 4)
             nc.vector.reciprocal(out=rz[:, cols], in_=zc[:, cols])
 
         def stage_factor(k):
@@ -389,31 +397,36 @@ def tile_hyperbolicuniform_pa_t_kernel(tc, h_mlp, W3, b3, prototypes, out_0, out
                 stage_transpose(s + LQ + 1)
             if s + LQ < NS:
                 stage_copy(s + LQ)
+            odd = {}
+            for lag in range(LP3, LP3 + 6):
+                if 0 <= s - lag < NJ and (s - lag) % 2 == 1:
+                    odd[lag - LP3] = (s - lag) // 2
+            if 3 in odd:
+                stage_recip(odd[3])
             if s < NS:
                 stage_evacuate(s)
             if s + LQ < NS:
                 stage_quantise(s + LQ)
-            j = s - 1
-            if 0 <= j < NJ:
-                stage_norm(j)
-                if j % 2 == 1:
-                    stage_pow(j // 2)
-            j = s - 2
-            if 0 <= j < NJ and j % 2 == 1:
-                stage_tanh(j // 2)
-            j = s - 3
-            if 0 <= j < NJ and j % 2 == 1:
-                stage_factor(j // 2)
-                stage_scale(j // 2, 0)
-            j = s - 4
-            if 0 <= j < NJ and j % 2 == 1:
-                stage_scale(j // 2, 1)
+            if NJ <= s < NS:
+                stage_q(s)
+            if 0 <= s - LP3 < NJ:
+                stage_norm(s - LP3)
+            if 0 in odd:
+                stage_pow(odd[0])
+            if 2 in odd:
+                stage_tanh(odd[2])
+            if 3 in odd:
+                stage_factor(odd[3])
+            if 4 in odd:
+                stage_scale(odd[4], 0)
+            if 5 in odd:
+                stage_scale(odd[5], 1)
             k = (s - NJ - 2) // 2
             if (s - NJ) % 2 == 0 and k in VARB:
                 stage_pre(k)
-            if s == 15:
+            if s == 18:
                 stage_rowconst(0)
-            if s == 27:
+            if s == 30:
                 stage_rowconst(1)
             follow(1)
             credit = credit + (CD_CAP if s < NS else 100.0)

@@ -65,6 +65,8 @@ def tile_hyperbolicuniform_pa_t_kernel(tc, h_mlp, W3, b3, prototypes, out_0, out
         make_identity(nc, ident_bf[:])
         make_identity(nc, ident[:])
         nc.gpsimd.memset(half[:], 0.5)
+        mhalf = const.tile([P, 4], F32, name="mhalf")
+        nc.gpsimd.memset(mhalf[:], -0.5)
 
         bias_bc = const.tile([P, D], BF16, name="bias_bc")
         pr = const.tile([P, 2, D], BF16, name="pr")
@@ -286,19 +288,16 @@ def tile_hyperbolicuniform_pa_t_kernel(tc, h_mlp, W3, b3, prototypes, out_0, out
             cols = slice(4 * k, 4 * k + 4)
             src = zzv if k in P3V_Q else zz
             nc.gpsimd.tensor_tensor(out=zt[:, cols], in0=src[:, cols], in1=half[:], op=ALU.pow)
+            nc.gpsimd.tensor_scalar(out=zc[:, cols], in0=src[:, cols], scalar1=ZMIN * ZMIN, scalar2=None, op0=ALU.max)
+            nc.gpsimd.tensor_tensor(out=rz[:, cols], in0=zc[:, cols], in1=mhalf[:], op=ALU.pow)
 
         def stage_tanh(k):
             cols = slice(4 * k, 4 * k + 4)
             nc.scalar.activation(out=th[:, cols], in_=zt[:, cols], func=ACT.Tanh)
-            nc.vector.tensor_scalar(out=zc[:, cols], in0=zt[:, cols], scalar1=ZMIN, scalar2=None, op0=ALU.max)
-
-        def stage_recip(k):
-            cols = slice(4 * k, 4 * k + 4)
-            nc.vector.reciprocal(out=rz[:, cols], in_=zc[:, cols])
 
         def stage_factor(k):
             cols = slice(4 * k, 4 * k + 4)
-            nc.vector.tensor_tensor(out=fs[:, cols], in0=th[:, cols], in1=rz[:, cols], op=ALU.mult)
+            nc.gpsimd.tensor_tensor(out=fs[:, cols], in0=th[:, cols], in1=rz[:, cols], op=ALU.mult)
 
         def stage_scale(k, part):
             for t in (4 * k + 2 * part, 4 * k + 2 * part + 1):
@@ -401,8 +400,6 @@ def tile_hyperbolicuniform_pa_t_kernel(tc, h_mlp, W3, b3, prototypes, out_0, out
             for lag in range(LP3, LP3 + 6):
                 if 0 <= s - lag < NJ and (s - lag) % 2 == 1:
                     odd[lag - LP3] = (s - lag) // 2
-            if 3 in odd:
-                stage_recip(odd[3])
             if s < NS:
                 stage_evacuate(s)
             if s + LQ < NS:

@@ -31,10 +31,10 @@ LP3 = 2
 CYCLES = (9, 3)
 CD_DELAY = 2
 CD_CAP = 2.0
-C1_V = (5, 7, 9, 11, 13, 15)
+C1_V = (5, 7, 9, 11, 13, 15, 21, 27, 33, 39, 45)
 P3V_Q = ()
 P6_V = (33, 37, 41, 45)
-P4_G = ()
+P4_G = tuple(range(1, 48, 2))
 O5_G = ()
 VARB = (10, 11)
 R1_BUFS = 6
@@ -61,10 +61,8 @@ def tile_hyperbolicuniform_pa_t_kernel(tc, h_mlp, W3, b3, prototypes, out_0, out
 
         ident = const.tile([P, P], F32, name="ident")
         ident_bf = const.tile([P, P], BF16, name="ident_bf")
-        half = const.tile([P, 4], F32, name="half")
         make_identity(nc, ident_bf[:])
         make_identity(nc, ident[:])
-        nc.gpsimd.memset(half[:], 0.5)
         mhalf = const.tile([P, 4], F32, name="mhalf")
         nc.gpsimd.memset(mhalf[:], -0.5)
 
@@ -287,9 +285,9 @@ def tile_hyperbolicuniform_pa_t_kernel(tc, h_mlp, W3, b3, prototypes, out_0, out
         def stage_pow(k):
             cols = slice(4 * k, 4 * k + 4)
             src = zzv if k in P3V_Q else zz
-            nc.gpsimd.tensor_tensor(out=zt[:, cols], in0=src[:, cols], in1=half[:], op=ALU.pow)
             nc.gpsimd.tensor_scalar(out=zc[:, cols], in0=src[:, cols], scalar1=ZMIN * ZMIN, scalar2=None, op0=ALU.max)
             nc.gpsimd.tensor_tensor(out=rz[:, cols], in0=zc[:, cols], in1=mhalf[:], op=ALU.pow)
+            nc.gpsimd.tensor_tensor(out=zt[:, cols], in0=src[:, cols], in1=rz[:, cols], op=ALU.mult)
 
         def stage_tanh(k):
             cols = slice(4 * k, 4 * k + 4)

@@ -28,13 +28,14 @@ GAMMA_MIN = 1e-10
 
 LQ = 2
 LP3 = 2
+LC = 1
 CYCLES = (9, 3)
-CD_DELAY = 2
+CD_DELAY = 3
 CD_CAP = 2.0
-C1_V = (5, 7, 9, 11, 13, 15, 21, 27, 33, 39, 45)
+C1_V = (5, 7, 9, 11, 13, 15)
 P3V_Q = ()
-P6_V = (33, 37, 41, 45)
-P4_G = tuple(range(1, 48, 2))
+P6_V = (1, 3, 5, 33, 37, 41, 45)
+P4_G = ()
 O5_G = ()
 VARB = (10, 11)
 R1_BUFS = 6
@@ -61,8 +62,10 @@ def tile_hyperbolicuniform_pa_t_kernel(tc, h_mlp, W3, b3, prototypes, out_0, out
 
         ident = const.tile([P, P], F32, name="ident")
         ident_bf = const.tile([P, P], BF16, name="ident_bf")
+        half = const.tile([P, 4], F32, name="half")
         make_identity(nc, ident_bf[:])
         make_identity(nc, ident[:])
+        nc.gpsimd.memset(half[:], 0.5)
         mhalf = const.tile([P, 4], F32, name="mhalf")
         nc.gpsimd.memset(mhalf[:], -0.5)
 
@@ -91,7 +94,8 @@ def tile_hyperbolicuniform_pa_t_kernel(tc, h_mlp, W3, b3, prototypes, out_0, out
                 in_=W3[512 * g : 512 * (g + 1), :].rearrange("(u p e) d -> p u e d", u=2, e=2),
             )
         load_h(0, parts=2)
-        for k in range(1, 4):
+        load_h(1, parts=2)
+        for k in range(2, 4):
             load_h(k)
 
         def regroup_w(g):
@@ -285,9 +289,9 @@ def tile_hyperbolicuniform_pa_t_kernel(tc, h_mlp, W3, b3, prototypes, out_0, out
         def stage_pow(k):
             cols = slice(4 * k, 4 * k + 4)
             src = zzv if k in P3V_Q else zz
+            nc.gpsimd.tensor_tensor(out=zt[:, cols], in0=src[:, cols], in1=half[:], op=ALU.pow)
             nc.gpsimd.tensor_scalar(out=zc[:, cols], in0=src[:, cols], scalar1=ZMIN * ZMIN, scalar2=None, op0=ALU.max)
             nc.gpsimd.tensor_tensor(out=rz[:, cols], in0=zc[:, cols], in1=mhalf[:], op=ALU.pow)
-            nc.gpsimd.tensor_tensor(out=zt[:, cols], in0=src[:, cols], in1=rz[:, cols], op=ALU.mult)
 
         def stage_tanh(k):
             cols = slice(4 * k, 4 * k + 4)
@@ -304,8 +308,9 @@ def tile_hyperbolicuniform_pa_t_kernel(tc, h_mlp, W3, b3, prototypes, out_0, out
                     nc.gpsimd.tensor_scalar(out=u, in0=u, scalar1=fs[:, t : t + 1], scalar2=0.0, op0=ALU.mult, op1=ALU.add)
                 else:
                     nc.vector.tensor_scalar(out=u, in0=u, scalar1=fs[:, t : t + 1], scalar2=None, op0=ALU.mult)
-            if part == 1:
-                nc.sync.dma_start(out=hyp_v[:, 4 * k : 4 * k + 4, :], in_=ub_tiles[k][:])
+
+        def store_hyp(k):
+            nc.sync.dma_start(out=hyp_v[:, 4 * k : 4 * k + 4, :], in_=ub_tiles[k][:])
 
         def stage_rowconst(part):
             cols = slice(24 * part, 24 * (part + 1))
@@ -378,10 +383,11 @@ def tile_hyperbolicuniform_pa_t_kernel(tc, h_mlp, W3, b3, prototypes, out_0, out
                 else:
                     stage_out(k)
 
-        for J in range(LQ + 1):
+        for J in range(LQ + LC + 1):
             stage_transpose(J)
-            if J < LQ:
+            if J < LQ + LC:
                 stage_copy(J)
+            if J < LQ:
                 stage_quantise(J)
 
         NS = 2 * NJ
@@ -390,10 +396,10 @@ def tile_hyperbolicuniform_pa_t_kernel(tc, h_mlp, W3, b3, prototypes, out_0, out
         while s < NS or done[1] < len(items) or done[0] < len(pend):
             if s < NS:
                 stage_mx(s)
-            if s + LQ + 1 < NS:
-                stage_transpose(s + LQ + 1)
-            if s + LQ < NS:
-                stage_copy(s + LQ)
+            if s + LQ + LC + 1 < NS:
+                stage_transpose(s + LQ + LC + 1)
+            if s + LQ + LC < NS:
+                stage_copy(s + LQ + LC)
             odd = {}
             for lag in range(LP3, LP3 + 6):
                 if 0 <= s - lag < NJ and (s - lag) % 2 == 1:
@@ -416,6 +422,8 @@ def tile_hyperbolicuniform_pa_t_kernel(tc, h_mlp, W3, b3, prototypes, out_0, out
                 stage_scale(odd[4], 0)
             if 5 in odd:
                 stage_scale(odd[5], 1)
+            if s >= LP3 + 6 and (s - LP3 - 6) % 3 == 0 and (s - LP3 - 6) // 3 < NQ:
+                store_hyp((s - LP3 - 6) // 3)
             k = (s - NJ - 2) // 2
             if (s - NJ) % 2 == 0 and k in VARB:
                 stage_pre(k)

@@ -28,13 +28,12 @@ GAMMA_MIN = 1e-10
 
 LQ = 2
 LP3 = 2
-LC = 1
 CYCLES = (9, 3)
-CD_DELAY = 3
+CD_DELAY = 2
 CD_CAP = 2.0
 C1_V = (5, 7, 9, 11, 13, 15)
 P3V_Q = ()
-P6_V = (1, 3, 5, 33, 37, 41, 45)
+P6_V = (33, 37, 41, 45)
 P4_G = ()
 O5_G = ()
 VARB = (10, 11)
@@ -63,16 +62,20 @@ def tile_hyperbolicuniform_pa_t_kernel(tc, h_mlp, W3, b3, prototypes, out_0, out
         ident = const.tile([P, P], F32, name="ident")
         ident_bf = const.tile([P, P], BF16, name="ident_bf")
         half = const.tile([P, 4], F32, name="half")
+        bias_row = const.tile([P, D], BF16, name="bias_row")
+        ones = const.tile([P, P], BF16, name="ones")
+        nc.gpsimd.memset(bias_row[:], 0.0)
         make_identity(nc, ident_bf[:])
         make_identity(nc, ident[:])
+        nc.gpsimd.memset(ones[:], 1.0)
         nc.gpsimd.memset(half[:], 0.5)
         mhalf = const.tile([P, 4], F32, name="mhalf")
         nc.gpsimd.memset(mhalf[:], -0.5)
 
-        bias_bc = const.tile([P, D], BF16, name="bias_bc")
+        bias_bc = const.tile([P, D], F32, name="bias_bc")
         pr = const.tile([P, 2, D], BF16, name="pr")
         nc.scalar.dma_start(out=pr[:], in_=prototypes.rearrange("(c p) d -> p c d", c=2))
-        nc.scalar.dma_start(out=bias_bc[:], in_=b3.partition_broadcast(P))
+        nc.scalar.dma_start(out=bias_row[0:1, :], in_=b3.unsqueeze(0))
 
         h_tiles = {}
 
@@ -94,8 +97,7 @@ def tile_hyperbolicuniform_pa_t_kernel(tc, h_mlp, W3, b3, prototypes, out_0, out
                 in_=W3[512 * g : 512 * (g + 1), :].rearrange("(u p e) d -> p u e d", u=2, e=2),
             )
         load_h(0, parts=2)
-        load_h(1, parts=2)
-        for k in range(2, 4):
+        for k in range(1, 4):
             load_h(k)
 
         def regroup_w(g):
@@ -153,9 +155,12 @@ def tile_hyperbolicuniform_pa_t_kernel(tc, h_mlp, W3, b3, prototypes, out_0, out
             nc.tensor.matmul(
                 out=psb[:, m, :], lhsT=hv[:, m : m + 1].to_broadcast([P, P]), rhs=ident[:], start=True, stop=True
             )
+        psbias = mm.tile([P, D], F32, name="psbias", tag="mm")
+        nc.tensor.matmul(out=psbias[:], lhsT=ones[:], rhs=bias_row[:], start=True, stop=True)
         for c in range(2):
             nc.scalar.copy(out=pg[:, P * c : P * (c + 1), :], in_=proto_ps[c][:].rearrange("p t j -> p j t"))
         nc.scalar.copy(out=haib[:].rearrange("p v j -> p (v j)"), in_=psb[:].rearrange("p m j -> p (m j)"))
+        nc.scalar.copy(out=bias_bc[:], in_=psbias[:])
         quantise_w(1)
         nc.vector.quantize_mx(out=pc[:].bitcast(FP8X4), scales=psc[:], in_=pg[:].rearrange("p j t -> p (j t)"))
 
@@ -308,18 +313,24 @@ def tile_hyperbolicuniform_pa_t_kernel(tc, h_mlp, W3, b3, prototypes, out_0, out
                     nc.gpsimd.tensor_scalar(out=u, in0=u, scalar1=fs[:, t : t + 1], scalar2=0.0, op0=ALU.mult, op1=ALU.add)
                 else:
                     nc.vector.tensor_scalar(out=u, in0=u, scalar1=fs[:, t : t + 1], scalar2=None, op0=ALU.mult)
+            if part == 1:
+                nc.sync.dma_start(out=hyp_v[:, 4 * k : 4 * k + 4, :], in_=ub_tiles[k][:])
 
-        def store_hyp(k):
-            nc.sync.dma_start(out=hyp_v[:, 4 * k : 4 * k + 4, :], in_=ub_tiles[k][:])
-
-        def stage_rowconst(part):
+        def stage_rowconst(part, sub):
             cols = slice(24 * part, 24 * (part + 1))
-            nc.vector.tensor_tensor(out=cb[:, cols], in0=th[:, cols], in1=th[:, cols], op=ALU.mult)
-            nc.vector.tensor_scalar(out=gm[:, cols], in0=cb[:, cols], scalar1=-1.0, scalar2=1.0, op0=ALU.mult, op1=ALU.add)
-            nc.vector.tensor_scalar(out=hb[:, cols], in0=cb[:, cols], scalar1=0.5 / C, scalar2=None, op0=ALU.mult)
-            nc.vector.tensor_scalar(out=gc[:, cols], in0=gm[:, cols], scalar1=GAMMA_MIN, scalar2=None, op0=ALU.max)
-            nc.vector.reciprocal(out=ig[:, cols], in_=gc[:, cols])
-            nc.vector.tensor_scalar(out=sv[:, cols], in0=ig[:, cols], scalar1=-2.0 * C, scalar2=None, op0=ALU.mult)
+            if sub == 0:
+                nc.vector.tensor_tensor(out=cb[:, cols], in0=th[:, cols], in1=th[:, cols], op=ALU.mult)
+            elif sub == 1:
+                nc.vector.tensor_scalar(
+                    out=gm[:, cols], in0=cb[:, cols], scalar1=-1.0, scalar2=1.0, op0=ALU.mult, op1=ALU.add
+                )
+                nc.vector.tensor_scalar(out=hb[:, cols], in0=cb[:, cols], scalar1=0.5 / C, scalar2=None, op0=ALU.mult)
+            elif sub == 2:
+                nc.vector.tensor_scalar(out=gc[:, cols], in0=gm[:, cols], scalar1=GAMMA_MIN, scalar2=None, op0=ALU.max)
+            elif sub == 3:
+                nc.vector.reciprocal(out=ig[:, cols], in_=gc[:, cols])
+            elif sub == 4:
+                nc.vector.tensor_scalar(out=sv[:, cols], in0=ig[:, cols], scalar1=-2.0 * C, scalar2=None, op0=ALU.mult)
 
         def flat_q(k):
             return q_tiles[k][:].rearrange("p i j -> p (i j)")
@@ -352,18 +363,25 @@ def tile_hyperbolicuniform_pa_t_kernel(tc, h_mlp, W3, b3, prototypes, out_0, out
                     out=flat_q(k), in0=flat_q(k), scalar=0.0, in1=r1_tiles[k][:], op0=ALU.max, op1=ALU.add
                 )
 
+        def pieces(k):
+            return ((0, 2), (2, 2)) if k == NQ - 1 else ((0, 4),)
+
         def stage_ln(k):
-            if k in VARB:
-                nc.scalar.activation(out=flat_q(k), in_=flat_q(k), func=ACT.Ln, scale=2.0, bias=1.0)
-            else:
-                nc.scalar.activation(out=flat_q(k), in_=flat_q(k), func=ACT.Ln)
+            for a, n in pieces(k):
+                v = q_tiles[k][:, a : a + n, :].rearrange("p i j -> p (i j)")
+                if k in VARB:
+                    nc.scalar.activation(out=v, in_=v, func=ACT.Ln, scale=2.0, bias=1.0)
+                else:
+                    nc.scalar.activation(out=v, in_=v, func=ACT.Ln)
 
         def stage_out(k):
-            nc.vector.tensor_scalar(
-                out=flat_q(k), in0=flat_q(k), scalar1=(-KLOG if k in VARB else -2.0 * KLOG), scalar2=-KLOG * LOG_RMAX,
-                op0=ALU.mult, op1=ALU.max,
-            )
-            nc.sync.dma_start(out=log_v[:, 4 * k : 4 * k + 4, :], in_=q_tiles[k][:])
+            for a, n in pieces(k):
+                v = q_tiles[k][:, a : a + n, :].rearrange("p i j -> p (i j)")
+                nc.vector.tensor_scalar(
+                    out=v, in0=v, scalar1=(-KLOG if k in VARB else -2.0 * KLOG), scalar2=-KLOG * LOG_RMAX,
+                    op0=ALU.mult, op1=ALU.max,
+                )
+                nc.sync.dma_start(out=log_v[:, 4 * k + a : 4 * k + a + n, :], in_=q_tiles[k][:, a : a + n, :])
 
         items = []
         a = 0
@@ -383,11 +401,10 @@ def tile_hyperbolicuniform_pa_t_kernel(tc, h_mlp, W3, b3, prototypes, out_0, out
                 else:
                     stage_out(k)
 
-        for J in range(LQ + LC + 1):
+        for J in range(LQ + 1):
             stage_transpose(J)
-            if J < LQ + LC:
-                stage_copy(J)
             if J < LQ:
+                stage_copy(J)
                 stage_quantise(J)
 
         NS = 2 * NJ
@@ -396,10 +413,10 @@ def tile_hyperbolicuniform_pa_t_kernel(tc, h_mlp, W3, b3, prototypes, out_0, out
         while s < NS or done[1] < len(items) or done[0] < len(pend):
             if s < NS:
                 stage_mx(s)
-            if s + LQ + LC + 1 < NS:
-                stage_transpose(s + LQ + LC + 1)
-            if s + LQ + LC < NS:
-                stage_copy(s + LQ + LC)
+            if s + LQ + 1 < NS:
+                stage_transpose(s + LQ + 1)
+            if s + LQ < NS:
+                stage_copy(s + LQ)
             odd = {}
             for lag in range(LP3, LP3 + 6):
                 if 0 <= s - lag < NJ and (s - lag) % 2 == 1:
@@ -422,15 +439,13 @@ def tile_hyperbolicuniform_pa_t_kernel(tc, h_mlp, W3, b3, prototypes, out_0, out
                 stage_scale(odd[4], 0)
             if 5 in odd:
                 stage_scale(odd[5], 1)
-            if s >= LP3 + 6 and (s - LP3 - 6) % 3 == 0 and (s - LP3 - 6) // 3 < NQ:
-                store_hyp((s - LP3 - 6) // 3)
             k = (s - NJ - 2) // 2
             if (s - NJ) % 2 == 0 and k in VARB:
                 stage_pre(k)
-            if s == 18:
-                stage_rowconst(0)
-            if s == 30:
-                stage_rowconst(1)
+            if 18 <= s < 23:
+                stage_rowconst(0, s - 18)
+            if 30 <= s < 35:
+                stage_rowconst(1, s - 30)
             follow(1)
             credit = credit + (CD_CAP if s < NS else 100.0)
             while done[1] < len(items):

@@ -16,455 +16,442 @@ B, H, D, N = 6144, 1024, 512, 256
 FLOPS = 2 * B * H * D + 2 * B * D * N
 
 P = 128
-NT = B // P
-NQ = NT // 4
-NJ = NT // 2
+TILES = B // P
+PAIRS = TILES // 2
+QUADS = TILES // 4
+JOBS = 2 * PAIRS
+K_PASS = 4 * P
+
 C = 3.0
 SQRT_C = math.sqrt(C)
-KLOG = 1.0 / (0.07 * SQRT_C)
-LOG_RMAX = math.log((2.0 - 1e-5) / 1e-5)
-ZMIN = SQRT_C * 1e-15
+K_LOGIT = 1.0 / (0.07 * SQRT_C)
+LOGIT_MIN = -K_LOGIT * math.log((2.0 - 1e-5) / 1e-5)
+Z_MIN = SQRT_C * 1e-15
 GAMMA_MIN = 1e-10
 
-LQ = 2
-LP3 = 2
-CYCLES = (9, 3)
-CD_DELAY = 2
-CD_CAP = 2.0
-C1_V = (5, 7, 9, 11, 13, 15)
-P3V_Q = ()
-P6_V = (33, 37, 41, 45)
-P4_G = ()
-O5_G = ()
-VARB = (10, 11)
-R1_BUFS = 6
+QUANTISE_AHEAD = 2
+NORM_BEHIND = 2
+TANH_BEHIND = NORM_BEHIND + 2
+FACTOR_BEHIND = NORM_BEHIND + 3
+SCALE_BEHIND = NORM_BEHIND + 4
+ROOTS_BEHIND = 2
+
+ROOT_LOG_RUNS = (9, 3)
+SECOND_FORM = (10, 11)
+SCALAR_PASSES_A_STEP = 2
+
+H_COPIES_ON_VECTOR = (5, 7, 9, 11, 13, 15)
+HYP_COPIES_ON_VECTOR = (33, 37, 41, 45)
 
 
 def tile_hyperbolicuniform_pa_t_kernel(tc, h_mlp, W3, b3, prototypes, out_0, out_1):
     nc = tc.nc
-    h_v = h_mlp.rearrange("(p n) k -> p n k", n=NT)
-    hyp_v = out_1.rearrange("(p n) d -> p n d", n=NT)
-    log_v = out_0.rearrange("(p n) j -> p n j", n=NT)
+    h_rows = h_mlp.rearrange("(p t) k -> p t k", t=TILES)
+    hyp_rows = out_1.rearrange("(p t) d -> p t d", t=TILES)
+    logit_rows = out_0.rearrange("(p t) j -> p t j", t=TILES)
 
     with ExitStack() as ctx:
         ctx.enter_context(tc.manual_schedule())
         const = ctx.enter_context(tc.tile_pool(name="const", bufs=1))
-        hpool = ctx.enter_context(tc.tile_pool(name="hpool", bufs=4))
-        ubpool = ctx.enter_context(tc.tile_pool(name="ubpool", bufs=NQ))
-        grp = ctx.enter_context(tc.tile_pool(name="grp", bufs=4))
-        cod = ctx.enter_context(tc.tile_pool(name="cod", bufs=4))
-        r1pool = ctx.enter_context(tc.tile_pool(name="r1pool", bufs=R1_BUFS))
-        epool = ctx.enter_context(tc.tile_pool(name="epool", bufs=4))
-        junkp = ctx.enter_context(tc.tile_pool(name="junkp", bufs=4))
-        tp = ctx.enter_context(tc.psum_pool(name="tp", bufs=4))
-        mm = ctx.enter_context(tc.psum_pool(name="mm", bufs=4))
+        h_pool = ctx.enter_context(tc.tile_pool(name="h_pool", bufs=4))
+        row_pool = ctx.enter_context(tc.tile_pool(name="row_pool", bufs=QUADS))
+        mx_pool = ctx.enter_context(tc.tile_pool(name="mx_pool", bufs=4))
+        dist_pool = ctx.enter_context(tc.tile_pool(name="dist_pool", bufs=4))
+        aux_pool = ctx.enter_context(tc.tile_pool(name="aux_pool", bufs=6))
+        tr_psum = ctx.enter_context(tc.psum_pool(name="tr_psum", bufs=4))
+        mm_psum = ctx.enter_context(tc.psum_pool(name="mm_psum", bufs=4))
 
         ident = const.tile([P, P], F32, name="ident")
         ident_bf = const.tile([P, P], BF16, name="ident_bf")
-        half = const.tile([P, 4], F32, name="half")
         bias_row = const.tile([P, D], BF16, name="bias_row")
         ones = const.tile([P, P], BF16, name="ones")
+        minus_half = const.tile([P, 4], F32, name="minus_half")
         nc.gpsimd.memset(bias_row[:], 0.0)
         make_identity(nc, ident_bf[:])
-        make_identity(nc, ident[:])
         nc.gpsimd.memset(ones[:], 1.0)
-        nc.gpsimd.memset(half[:], 0.5)
-        mhalf = const.tile([P, 4], F32, name="mhalf")
-        nc.gpsimd.memset(mhalf[:], -0.5)
+        make_identity(nc, ident[:])
+        nc.gpsimd.memset(minus_half[:], -0.5)
 
-        bias_bc = const.tile([P, D], F32, name="bias_bc")
-        pr = const.tile([P, 2, D], BF16, name="pr")
-        nc.scalar.dma_start(out=pr[:], in_=prototypes.rearrange("(c p) d -> p c d", c=2))
+        proto = const.tile([P, 2, D], BF16, name="proto")
+        nc.scalar.dma_start(out=proto[:], in_=prototypes.rearrange("(c p) d -> p c d", c=2))
         nc.scalar.dma_start(out=bias_row[0:1, :], in_=b3.unsqueeze(0))
 
-        h_tiles = {}
-
-        def load_h(k, parts=1):
-            ht = hpool.tile([P, 4, H], BF16, name="h_sb", tag="h_sb")
-            h_tiles[k] = ht
-            step = 4 // parts
-            for a in range(0, 4, step):
-                nc.sync.dma_start(out=ht[:, a : a + step, :], in_=h_v[:, 4 * k + a : 4 * k + a + step, :])
-
         w_raw = const.tile([P, 2, 2, 2, D], BF16, name="w_raw")
-        wg = const.tile([P, 2, D, 4], BF16, name="wg", align_bytes=64)
-        wc = const.tile([P, 2, D], U32, name="wc", align_bytes=64)
-        ws = const.tile([P, 2, D], U8, name="ws", align_bytes=64)
-
+        w_grouped = const.tile([P, 2, D, 4], BF16, name="w_grouped", align_bytes=64)
+        w_codes = const.tile([P, 2, D], U32, name="w_codes", align_bytes=64)
+        w_scales = const.tile([P, 2, D], U8, name="w_scales", align_bytes=64)
         for g in range(2):
             nc.sync.dma_start(
                 out=w_raw[:, g],
-                in_=W3[512 * g : 512 * (g + 1), :].rearrange("(u p e) d -> p u e d", u=2, e=2),
+                in_=W3[K_PASS * g : K_PASS * (g + 1), :].rearrange("(u p e) d -> p u e d", u=2, e=2),
             )
-        load_h(0, parts=2)
-        for k in range(1, 4):
-            load_h(k)
+
+        h_quads = {}
+
+        def load_h(k, pieces):
+            h_quads[k] = h_pool.tile([P, 4, H], BF16, name="h_quad", tag="h_quad")
+            n = 4 // pieces
+            for a in range(0, 4, n):
+                nc.sync.dma_start(out=h_quads[k][:, a : a + n, :], in_=h_rows[:, 4 * k + a : 4 * k + a + n, :])
+
+        load_h(0, 2)
+        load_h(1, 2)
+        load_h(2, 1)
+        load_h(3, 1)
 
         def regroup_w(g):
             nc.vector.tensor_copy(
-                out=wg[:, g].rearrange("p (c i) t -> p c t i", i=4),
+                out=w_grouped[:, g].rearrange("p (c i) t -> p c t i", i=4),
                 in_=w_raw[:, g].rearrange("p u e (c i) -> p c (u e) i", i=4),
             )
 
         def quantise_w(g):
             nc.vector.quantize_mx(
-                out=wc[:, g, :].bitcast(FP8X4),
-                scales=ws[:, g, :],
-                in_=wg[:, g].rearrange("p d t -> p (d t)"),
+                out=w_codes[:, g, :].bitcast(FP8X4),
+                scales=w_scales[:, g, :],
+                in_=w_grouped[:, g].rearrange("p d t -> p (d t)"),
             )
 
-        zz = const.tile([P, NT], F32, name="zz")
-        zzv = const.tile([P, NT], F32, name="zzv")
-        zt = const.tile([P, NT], F32, name="zt")
-        th = const.tile([P, NT], F32, name="th")
-        zc = const.tile([P, NT], F32, name="zc")
-        rz = const.tile([P, NT], F32, name="rz")
-        fs = const.tile([P, NT], F32, name="fs")
-        cb = const.tile([P, NT], F32, name="cb")
-        hb = const.tile([P, NT], F32, name="hb")
-        gm = const.tile([P, NT], F32, name="gm")
-        gc = const.tile([P, NT], F32, name="gc")
-        ig = const.tile([P, NT], F32, name="ig")
-        sv = const.tile([P, NT], F32, name="sv")
-        junk = const.tile([P, D], BF16, name="junk")
+        zz = const.tile([P, TILES], F32, name="zz")
+        tanh_z = const.tile([P, TILES], F32, name="tanh_z")
+        zz_floor = const.tile([P, TILES], F32, name="zz_floor")
+        z_inv = const.tile([P, TILES], F32, name="z_inv")
+        z = const.tile([P, TILES], F32, name="z")
+        factor = const.tile([P, TILES], F32, name="factor")
+        c_bn = const.tile([P, TILES], F32, name="c_bn")
+        half_bn = const.tile([P, TILES], F32, name="half_bn")
+        gamma = const.tile([P, TILES], F32, name="gamma")
+        gamma_floor = const.tile([P, TILES], F32, name="gamma_floor")
+        gamma_inv = const.tile([P, TILES], F32, name="gamma_inv")
+        row_scale = const.tile([P, TILES], F32, name="row_scale")
 
-        a2 = const.tile([P, 2], F32, name="a2")
-        bt = const.tile([P, 2], F32, name="bt")
-        hv = const.tile([P, 4], F32, name="hv")
-        pg = const.tile([P, N, 4], BF16, name="pg", align_bytes=64)
-        pc = const.tile([P, N], U32, name="pc", align_bytes=64)
-        psc = const.tile([P, N], U8, name="psc", align_bytes=64)
-        haib = const.tile([P, 2, N], F32, name="haib")
-        proto_ps = {}
+        a_col = const.tile([P, 2], F32, name="a_col")
+        beta_col = const.tile([P, 2], F32, name="beta_col")
+        col_consts = const.tile([P, 4], F32, name="col_consts")
+        proto_grouped = const.tile([P, N, 4], BF16, name="proto_grouped", align_bytes=64)
+        proto_codes = const.tile([P, N], U32, name="proto_codes", align_bytes=64)
+        proto_scales = const.tile([P, N], U8, name="proto_scales", align_bytes=64)
+        col_bc = const.tile([P, 2, N], F32, name="col_bc")
+        bias_bc = const.tile([P, D], F32, name="bias_bc")
+        proto_squares = const.tile([P, D], BF16, name="proto_squares")
 
         for c in range(2):
-            nc.scalar.activation(out=junk[:], in_=pr[:, c, :], func=ACT.Square, accum_out=a2[:, c : c + 1])
+            nc.scalar.activation(
+                out=proto_squares[:], in_=proto[:, c, :], func=ACT.Square, accum_out=a_col[:, c : c + 1]
+            )
+        proto_t = []
         for c in range(2):
-            ps = mm.tile([P, 4, P], BF16, name="tpp", tag="mm")
-            proto_ps[c] = ps
+            proto_t.append(mm_psum.tile([P, 4, P], BF16, name="proto_t", tag="mm"))
             for t in range(4):
-                nc.tensor.transpose(ps[:, t, :], pr[:, c, P * t : P * (t + 1)], ident_bf[:])
+                nc.tensor.transpose(proto_t[c][:, t, :], proto[:, c, P * t : P * (t + 1)], ident_bf[:])
+        bias_ps = mm_psum.tile([P, D], F32, name="bias_ps", tag="mm")
+        nc.tensor.matmul(out=bias_ps[:], lhsT=ones[:], rhs=bias_row[:], start=True, stop=True)
         regroup_w(0)
-        nc.vector.tensor_scalar(out=hv[:, 0:2], in0=a2[:], scalar1=0.5, scalar2=None, op0=ALU.mult)
-        nc.vector.tensor_scalar(out=bt[:], in0=a2[:], scalar1=-C, scalar2=1.0, op0=ALU.mult, op1=ALU.add)
+        nc.vector.tensor_scalar(out=col_consts[:, 0:2], in0=a_col[:], scalar1=0.5, scalar2=None, op0=ALU.mult)
+        nc.vector.tensor_scalar(out=beta_col[:], in0=a_col[:], scalar1=-C, scalar2=1.0, op0=ALU.mult, op1=ALU.add)
         regroup_w(1)
-        nc.vector.reciprocal(out=hv[:, 2:4], in_=bt[:])
+        nc.vector.reciprocal(out=col_consts[:, 2:4], in_=beta_col[:])
         quantise_w(0)
-        psb = mm.tile([P, 4, P], F32, name="tpb", tag="mm")
-        for m in range(4):
-            nc.tensor.matmul(
-                out=psb[:, m, :], lhsT=hv[:, m : m + 1].to_broadcast([P, P]), rhs=ident[:], start=True, stop=True
-            )
-        psbias = mm.tile([P, D], F32, name="psbias", tag="mm")
-        nc.tensor.matmul(out=psbias[:], lhsT=ones[:], rhs=bias_row[:], start=True, stop=True)
         for c in range(2):
-            nc.scalar.copy(out=pg[:, P * c : P * (c + 1), :], in_=proto_ps[c][:].rearrange("p t j -> p j t"))
-        nc.scalar.copy(out=haib[:].rearrange("p v j -> p (v j)"), in_=psb[:].rearrange("p m j -> p (m j)"))
-        nc.scalar.copy(out=bias_bc[:], in_=psbias[:])
+            nc.scalar.copy(
+                out=proto_grouped[:, P * c : P * (c + 1), :], in_=proto_t[c][:].rearrange("p t j -> p j t")
+            )
+        nc.scalar.copy(out=bias_bc[:], in_=bias_ps[:])
         quantise_w(1)
-        nc.vector.quantize_mx(out=pc[:].bitcast(FP8X4), scales=psc[:], in_=pg[:].rearrange("p j t -> p (j t)"))
+        nc.vector.quantize_mx(
+            out=proto_codes[:].bitcast(FP8X4), scales=proto_scales[:], in_=proto_grouped[:].rearrange("p j t -> p (j t)")
+        )
 
-        ub_tiles = {}
-        q_tiles = {}
-        tp_tiles = {}
-        grp_tiles = {}
-        cod_tiles = {}
-        mm_tiles = {}
-        r1_tiles = {}
-        e_tiles = {}
+        def spread_col_consts():
+            col_ps = mm_psum.tile([P, 4, P], F32, name="col_ps", tag="mm")
+            for m in range(4):
+                nc.tensor.matmul(
+                    out=col_ps[:, m, :], lhsT=col_consts[:, m : m + 1].to_broadcast([P, P]), rhs=ident[:],
+                    start=True, stop=True,
+                )
+            nc.scalar.copy(out=col_bc[:].rearrange("p v j -> p (v j)"), in_=col_ps[:].rearrange("p m j -> p (m j)"))
 
-        def stage_transpose(J):
+        row_quads = {}
+        q_quads = {}
+        transposed = {}
+        grouped = {}
+        codes = {}
+        products = {}
+        diffs = {}
+        aux = {}
+
+        def row_tile(t):
+            return row_quads[t // 4][:, t % 4, :]
+
+        def transpose_job(J):
             for i in range(2):
                 t = 2 * J + i
-                ps = tp.tile([P, 4, P], F32, name="tps", tag="tp")
-                tp_tiles[t] = ps
-                if J < NJ:
-                    src = h_tiles[t // 4][:].bitcast(F32)[:, t % 4, :]
+                transposed[t] = tr_psum.tile([P, 4, P], F32, name="transposed", tag="tr")
+                if J < PAIRS:
+                    src = h_quads[t // 4][:].bitcast(F32)[:, t % 4, :]
                 else:
-                    src = ub_tiles[(t - NT) // 4][:, (t - NT) % 4, :]
+                    src = row_tile(t - TILES)
                 for c in range(4):
-                    nc.tensor.transpose(ps[:, c, :], src[:, P * c : P * (c + 1)], ident[:])
-            if J < NJ and J % 2 == 1 and J // 2 + 4 < NQ:
-                load_h(J // 2 + 4)
+                    nc.tensor.transpose(transposed[t][:, c, :], src[:, P * c : P * (c + 1)], ident[:])
+            if J < PAIRS and J % 2 == 1 and J // 2 + 4 < QUADS:
+                load_h(J // 2 + 4, 1)
 
-        def stage_copy(J):
-            if J < NJ:
-                g = grp.tile([P, 2, 2, P, 4], BF16, name="hgrp", tag="grp", align_bytes=64)
-                g32 = g[:].bitcast(F32)
+        def copy_out_job(J):
+            if J < PAIRS:
+                grouped[J] = mx_pool.tile([P, 2, 2, P, 4], BF16, name="h_grouped", tag="grouped", align_bytes=64)
                 for i in range(2):
                     t = 2 * J + i
-                    src = tp_tiles[t][:].rearrange("p (g u) b -> p g b u", u=2)
-                    if t in C1_V:
-                        nc.vector.tensor_copy(out=g32[:, i], in_=src)
+                    dst = grouped[J][:].bitcast(F32)[:, i]
+                    src = transposed[t][:].rearrange("p (g u) b -> p g b u", u=2)
+                    if t in H_COPIES_ON_VECTOR:
+                        nc.vector.tensor_copy(out=dst, in_=src)
                     else:
-                        nc.scalar.copy(out=g32[:, i], in_=src)
+                        nc.scalar.copy(out=dst, in_=src)
             else:
-                g = grp.tile([P, 2, P, 4], BF16, name="ygrp", tag="grp", align_bytes=64)
+                grouped[J] = mx_pool.tile([P, 2, P, 4], BF16, name="hyp_grouped", tag="grouped", align_bytes=64)
                 for i in range(2):
                     t = 2 * J + i
-                    src = tp_tiles[t][:].rearrange("p t b -> p b t")
-                    if (t - NT) in P6_V:
-                        nc.vector.tensor_copy(out=g[:, i], in_=src)
+                    src = transposed[t][:].rearrange("p t b -> p b t")
+                    if t - TILES in HYP_COPIES_ON_VECTOR:
+                        nc.vector.tensor_copy(out=grouped[J][:, i], in_=src)
                     else:
-                        nc.scalar.copy(out=g[:, i], in_=src)
-            grp_tiles[J] = g
+                        nc.scalar.copy(out=grouped[J][:, i], in_=src)
 
-        def stage_quantise(J):
-            width = 512 if J < NJ else 256
-            c = cod.tile([P, width], U32, name="codes", tag="codes", align_bytes=64)
-            s_ = cod.tile([P, width], U8, name="scales", tag="scales", align_bytes=64)
-            cod_tiles[J] = (c, s_)
-            g = grp_tiles[J]
-            flat = g[:].rearrange("p i g b t -> p (i g b t)") if J < NJ else g[:].rearrange("p i b t -> p (i b t)")
-            nc.vector.quantize_mx(out=c[:].bitcast(FP8X4), scales=s_[:], in_=flat)
+        def quantise_job(J):
+            words = 4 * P if J < PAIRS else 2 * P
+            codes[J] = (
+                mx_pool.tile([P, words], U32, name="codes", tag="codes", align_bytes=64),
+                mx_pool.tile([P, words], U8, name="scales", tag="scales", align_bytes=64),
+            )
+            if J < PAIRS:
+                flat = grouped[J][:].rearrange("p i g b t -> p (i g b t)")
+            else:
+                flat = grouped[J][:].rearrange("p i b t -> p (i b t)")
+            nc.vector.quantize_mx(out=codes[J][0][:].bitcast(FP8X4), scales=codes[J][1][:], in_=flat)
 
-        def stage_mx(J):
-            c, s_ = cod_tiles[J]
-            if J < NJ:
+        def multiply_job(J):
+            words, scales = codes[J]
+            if J < PAIRS:
                 for i in range(2):
-                    acc = mm.tile([P, D], F32, name="acc", tag="mm")
-                    mm_tiles[2 * J + i] = acc
+                    products[2 * J + i] = mm_psum.tile([P, D], F32, name="u_ps", tag="mm")
                     for g in range(2):
-                        cols = slice(256 * i + P * g, 256 * i + P * (g + 1))
+                        cols = slice(P * (2 * i + g), P * (2 * i + g + 1))
                         nc.tensor.matmul_mx(
-                            out=acc[:],
-                            lhsT=c[:, cols].bitcast(FP8X4),
-                            lhsT_scale=s_[:, cols],
-                            rhs=wc[:, g, :].bitcast(FP8X4),
-                            rhs_scale=ws[:, g, :],
+                            out=products[2 * J + i][:],
+                            lhsT=words[:, cols].bitcast(FP8X4),
+                            lhsT_scale=scales[:, cols],
+                            rhs=w_codes[:, g, :].bitcast(FP8X4),
+                            rhs_scale=w_scales[:, g, :],
                             start=(g == 0),
                             stop=(g == 1),
                         )
             else:
-                acc = mm.tile([P, 2, N], F32, name="accx", tag="mm")
-                mm_tiles[2 * J] = acc
+                products[2 * J] = mm_psum.tile([P, 2, N], F32, name="x_ps", tag="mm")
                 for i in range(2):
                     cols = slice(P * i, P * (i + 1))
                     nc.tensor.matmul_mx(
-                        out=acc[:, i, :],
-                        lhsT=c[:, cols].bitcast(FP8X4),
-                        lhsT_scale=s_[:, cols],
-                        rhs=pc[:].bitcast(FP8X4),
-                        rhs_scale=psc[:],
+                        out=products[2 * J][:, i, :],
+                        lhsT=words[:, cols].bitcast(FP8X4),
+                        lhsT_scale=scales[:, cols],
+                        rhs=proto_codes[:].bitcast(FP8X4),
+                        rhs_scale=proto_scales[:],
                         start=True,
                         stop=True,
                     )
 
-        def stage_evacuate(J):
-            if J < NJ:
-                for i in range(2):
+        def leave_psum_job(J):
+            for i in range(2):
+                if J < PAIRS:
                     t = 2 * J + i
                     if t % 4 == 0:
-                        ub_tiles[t // 4] = ubpool.tile([P, 4, D], F32, name="ub", tag="ub")
-                    nc.vector.tensor_tensor(
-                        out=ub_tiles[t // 4][:, t % 4, :], in0=mm_tiles[t][:], in1=bias_bc[:], op=ALU.add
-                    )
-            else:
-                for i in range(2):
-                    t = 2 * (J - NJ) + i
-                    e = epool.tile([P, N], F32, name="e", tag="e")
-                    e_tiles[t] = e
+                        row_quads[t // 4] = row_pool.tile([P, 4, D], F32, name="row_quad", tag="quad")
+                    nc.vector.tensor_tensor(out=row_tile(t), in0=products[t][:], in1=bias_bc[:], op=ALU.add)
+                else:
+                    t = 2 * J + i - TILES
+                    diffs[t] = dist_pool.tile([P, N], F32, name="diff", tag="diff")
                     nc.vector.scalar_tensor_tensor(
-                        out=e[:], in0=mm_tiles[2 * J][:, i, :], scalar=hb[:, t : t + 1], in1=haib[:, 0, :],
+                        out=diffs[t][:], in0=products[2 * J][:, i, :], scalar=half_bn[:, t : t + 1], in1=col_bc[:, 0, :],
                         op0=ALU.subtract, op1=ALU.subtract,
                     )
 
-        def stage_q(J):
-            for i in range(2):
-                t = 2 * (J - NJ) + i
+        def q_job(J):
+            for t in (2 * J - TILES, 2 * J - TILES + 1):
                 if t % 4 == 0:
-                    q_tiles[t // 4] = ubpool.tile([P, 4, N], F32, name="q", tag="ub")
+                    q_quads[t // 4] = row_pool.tile([P, 4, N], F32, name="q_quad", tag="quad")
                 nc.vector.scalar_tensor_tensor(
-                    out=q_tiles[t // 4][:, t % 4, :], in0=e_tiles[t][:], scalar=sv[:, t : t + 1], in1=haib[:, 1, :],
+                    out=q_quads[t // 4][:, t % 4, :], in0=diffs[t][:], scalar=row_scale[:, t : t + 1], in1=col_bc[:, 1, :],
                     op0=ALU.mult, op1=ALU.mult,
                 )
 
-        def stage_norm(j):
+        def quad_cols(k):
+            return slice(4 * k, 4 * k + 4)
+
+        def norm_pair(j):
             for t in (2 * j, 2 * j + 1):
-                u = ub_tiles[t // 4][:, t % 4, :]
-                if t // 4 in P3V_Q:
-                    jk = junkp.tile([P, D], BF16, name="junkv", tag="junkv")
-                    nc.vector.scalar_tensor_tensor(
-                        out=jk[:], in0=u, scalar=C, in1=u, op0=ALU.mult, op1=ALU.mult, accum_out=zzv[:, t : t + 1]
-                    )
-                else:
-                    jk = junkp.tile([P, D], BF16, name="junks", tag="junks")
-                    nc.scalar.activation(out=jk[:], in_=u, func=ACT.Square, scale=SQRT_C, accum_out=zz[:, t : t + 1])
-
-        def stage_pow(k):
-            cols = slice(4 * k, 4 * k + 4)
-            src = zzv if k in P3V_Q else zz
-            nc.gpsimd.tensor_tensor(out=zt[:, cols], in0=src[:, cols], in1=half[:], op=ALU.pow)
-            nc.gpsimd.tensor_scalar(out=zc[:, cols], in0=src[:, cols], scalar1=ZMIN * ZMIN, scalar2=None, op0=ALU.max)
-            nc.gpsimd.tensor_tensor(out=rz[:, cols], in0=zc[:, cols], in1=mhalf[:], op=ALU.pow)
-
-        def stage_tanh(k):
-            cols = slice(4 * k, 4 * k + 4)
-            nc.scalar.activation(out=th[:, cols], in_=zt[:, cols], func=ACT.Tanh)
-
-        def stage_factor(k):
-            cols = slice(4 * k, 4 * k + 4)
-            nc.gpsimd.tensor_tensor(out=fs[:, cols], in0=th[:, cols], in1=rz[:, cols], op=ALU.mult)
-
-        def stage_scale(k, part):
-            for t in (4 * k + 2 * part, 4 * k + 2 * part + 1):
-                u = ub_tiles[k][:, t % 4, :]
-                if t in P4_G:
-                    nc.gpsimd.tensor_scalar(out=u, in0=u, scalar1=fs[:, t : t + 1], scalar2=0.0, op0=ALU.mult, op1=ALU.add)
-                else:
-                    nc.vector.tensor_scalar(out=u, in0=u, scalar1=fs[:, t : t + 1], scalar2=None, op0=ALU.mult)
-            if part == 1:
-                nc.sync.dma_start(out=hyp_v[:, 4 * k : 4 * k + 4, :], in_=ub_tiles[k][:])
-
-        def stage_rowconst(part, sub):
-            cols = slice(24 * part, 24 * (part + 1))
-            if sub == 0:
-                nc.vector.tensor_tensor(out=cb[:, cols], in0=th[:, cols], in1=th[:, cols], op=ALU.mult)
-            elif sub == 1:
-                nc.vector.tensor_scalar(
-                    out=gm[:, cols], in0=cb[:, cols], scalar1=-1.0, scalar2=1.0, op0=ALU.mult, op1=ALU.add
+                scratch = dist_pool.tile([P, D], BF16, name="scratch", tag="scratch")
+                nc.scalar.activation(
+                    out=scratch[:], in_=row_tile(t), func=ACT.Square, scale=SQRT_C, accum_out=zz[:, t : t + 1]
                 )
-                nc.vector.tensor_scalar(out=hb[:, cols], in0=cb[:, cols], scalar1=0.5 / C, scalar2=None, op0=ALU.mult)
-            elif sub == 2:
-                nc.vector.tensor_scalar(out=gc[:, cols], in0=gm[:, cols], scalar1=GAMMA_MIN, scalar2=None, op0=ALU.max)
-            elif sub == 3:
-                nc.vector.reciprocal(out=ig[:, cols], in_=gc[:, cols])
-            elif sub == 4:
-                nc.vector.tensor_scalar(out=sv[:, cols], in0=ig[:, cols], scalar1=-2.0 * C, scalar2=None, op0=ALU.mult)
 
-        def flat_q(k):
-            return q_tiles[k][:].rearrange("p i j -> p (i j)")
+        def root_of_norm_quad(k):
+            cols = quad_cols(k)
+            nc.gpsimd.tensor_scalar(out=zz_floor[:, cols], in0=zz[:, cols], scalar1=Z_MIN * Z_MIN, scalar2=None, op0=ALU.max)
+            nc.gpsimd.tensor_tensor(out=z_inv[:, cols], in0=zz_floor[:, cols], in1=minus_half[:], op=ALU.pow)
+            nc.gpsimd.tensor_tensor(out=z[:, cols], in0=zz[:, cols], in1=z_inv[:, cols], op=ALU.mult)
 
-        def stage_pre(k):
-            r1 = r1pool.tile([P, 4 * N], F32, name="r1", tag="r1")
-            r1_tiles[k] = r1
+        def tanh_quad(k):
+            nc.scalar.activation(out=tanh_z[:, quad_cols(k)], in_=z[:, quad_cols(k)], func=ACT.Tanh)
+
+        def factor_quad(k):
+            cols = quad_cols(k)
+            nc.gpsimd.tensor_tensor(out=factor[:, cols], in0=tanh_z[:, cols], in1=z_inv[:, cols], op=ALU.mult)
+
+        def scale_pair(j):
+            for t in (2 * j, 2 * j + 1):
+                nc.vector.tensor_scalar(
+                    out=row_tile(t), in0=row_tile(t), scalar1=factor[:, t : t + 1], scalar2=None, op0=ALU.mult
+                )
+
+        def store_hyp_quad(k):
+            nc.sync.dma_start(out=hyp_rows[:, 4 * k : 4 * k + 4, :], in_=row_quads[k][:])
+
+        def row_constants(half, link):
+            cols = slice(PAIRS * half, PAIRS * (half + 1))
+            if link == 0:
+                nc.vector.tensor_tensor(out=c_bn[:, cols], in0=tanh_z[:, cols], in1=tanh_z[:, cols], op=ALU.mult)
+            elif link == 1:
+                nc.vector.tensor_scalar(
+                    out=gamma[:, cols], in0=c_bn[:, cols], scalar1=-1.0, scalar2=1.0, op0=ALU.mult, op1=ALU.add
+                )
+                nc.vector.tensor_scalar(
+                    out=half_bn[:, cols], in0=c_bn[:, cols], scalar1=0.5 / C, scalar2=None, op0=ALU.mult
+                )
+            elif link == 2:
+                nc.vector.tensor_scalar(
+                    out=gamma_floor[:, cols], in0=gamma[:, cols], scalar1=GAMMA_MIN, scalar2=None, op0=ALU.max
+                )
+            elif link == 3:
+                nc.vector.reciprocal(out=gamma_inv[:, cols], in_=gamma_floor[:, cols])
+            else:
+                nc.vector.tensor_scalar(
+                    out=row_scale[:, cols], in0=gamma_inv[:, cols], scalar1=-2.0 * C, scalar2=None, op0=ALU.mult
+                )
+
+        def flat_q(k, first=0, tiles=4):
+            return q_quads[k][:, first : first + tiles, :].rearrange("p i j -> p (i j)")
+
+        def product_quad(k):
+            aux[k] = aux_pool.tile([P, 4 * N], F32, name="aux", tag="aux")
             nc.vector.scalar_tensor_tensor(
-                out=r1[:], in0=flat_q(k), scalar=1.0, in1=flat_q(k), op0=ALU.add, op1=ALU.mult
+                out=aux[k][:], in0=flat_q(k), scalar=1.0, in1=flat_q(k), op0=ALU.add, op1=ALU.mult
             )
 
-        def stage_sqrt(k):
-            if k in VARB:
-                nc.scalar.activation(out=r1_tiles[k][:], in_=r1_tiles[k][:], func=ACT.Sqrt)
+        def roots_quad(k):
+            if k in SECOND_FORM:
+                nc.scalar.activation(out=aux[k][:], in_=aux[k][:], func=ACT.Sqrt)
             else:
-                r1 = r1pool.tile([P, 4 * N], F32, name="r1", tag="r1")
-                r1_tiles[k] = r1
-                nc.scalar.activation(out=r1[:], in_=flat_q(k), func=ACT.Sqrt, bias=1.0)
+                aux[k] = aux_pool.tile([P, 4 * N], F32, name="aux", tag="aux")
+                nc.scalar.activation(out=aux[k][:], in_=flat_q(k), func=ACT.Sqrt, bias=1.0)
                 nc.scalar.activation(out=flat_q(k), in_=flat_q(k), func=ACT.Sqrt)
 
-        def stage_sum(k):
-            if k in VARB:
-                nc.vector.scalar_tensor_tensor(
-                    out=flat_q(k), in0=r1_tiles[k][:], scalar=0.0, in1=flat_q(k), op0=ALU.max, op1=ALU.add
-                )
-            elif k in O5_G:
-                nc.gpsimd.tensor_tensor(out=flat_q(k), in0=flat_q(k), in1=r1_tiles[k][:], op=ALU.add)
-            else:
-                nc.vector.scalar_tensor_tensor(
-                    out=flat_q(k), in0=flat_q(k), scalar=0.0, in1=r1_tiles[k][:], op0=ALU.max, op1=ALU.add
-                )
+        def sum_quad(k):
+            root, other = (aux[k][:], flat_q(k)) if k in SECOND_FORM else (flat_q(k), aux[k][:])
+            nc.vector.scalar_tensor_tensor(out=flat_q(k), in0=root, scalar=0.0, in1=other, op0=ALU.max, op1=ALU.add)
 
-        def pieces(k):
-            return ((0, 2), (2, 2)) if k == NQ - 1 else ((0, 4),)
+        def leaving_pieces(k):
+            return ((0, 2), (2, 2)) if k == QUADS - 1 else ((0, 4),)
 
-        def stage_ln(k):
-            for a, n in pieces(k):
-                v = q_tiles[k][:, a : a + n, :].rearrange("p i j -> p (i j)")
-                if k in VARB:
-                    nc.scalar.activation(out=v, in_=v, func=ACT.Ln, scale=2.0, bias=1.0)
+        def log_quad(k):
+            for first, tiles in leaving_pieces(k):
+                piece = flat_q(k, first, tiles)
+                if k in SECOND_FORM:
+                    nc.scalar.activation(out=piece, in_=piece, func=ACT.Ln, scale=2.0, bias=1.0)
                 else:
-                    nc.scalar.activation(out=v, in_=v, func=ACT.Ln)
+                    nc.scalar.activation(out=piece, in_=piece, func=ACT.Ln)
 
-        def stage_out(k):
-            for a, n in pieces(k):
-                v = q_tiles[k][:, a : a + n, :].rearrange("p i j -> p (i j)")
+        def finish_quad(k):
+            for first, tiles in leaving_pieces(k):
+                piece = flat_q(k, first, tiles)
                 nc.vector.tensor_scalar(
-                    out=v, in0=v, scalar1=(-KLOG if k in VARB else -2.0 * KLOG), scalar2=-KLOG * LOG_RMAX,
+                    out=piece, in0=piece, scalar1=(-K_LOGIT if k in SECOND_FORM else -2.0 * K_LOGIT), scalar2=LOGIT_MIN,
                     op0=ALU.mult, op1=ALU.max,
                 )
-                nc.sync.dma_start(out=log_v[:, 4 * k + a : 4 * k + a + n, :], in_=q_tiles[k][:, a : a + n, :])
+                nc.sync.dma_start(
+                    out=logit_rows[:, 4 * k + first : 4 * k + first + tiles, :],
+                    in_=q_quads[k][:, first : first + tiles, :],
+                )
 
-        items = []
-        a = 0
-        for n in CYCLES:
-            items.extend([("sqrt", k, NJ + 2 * k + 1 + CD_DELAY) for k in range(a, a + n)])
-            items.extend([("ln", k, NJ + 2 * k + 2 + CD_DELAY) for k in range(a, a + n)])
-            a += n
-        pend = []
-        done = [0, 0]
+        scalar_passes = []
+        first_quad = 0
+        for run in ROOT_LOG_RUNS:
+            quads = range(first_quad, first_quad + run)
+            scalar_passes.extend([(roots_quad, sum_quad, k) for k in quads])
+            scalar_passes.extend([(log_quad, finish_quad, k) for k in quads])
+            first_quad += run
 
-        def follow(keep):
-            while len(pend) - done[0] > keep:
-                kind, k = pend[done[0]]
-                done[0] += 1
-                if kind == "sqrt":
-                    stage_sum(k)
-                else:
-                    stage_out(k)
+        def quad_completed(step, behind):
+            j = step - behind
+            return j // 2 if 0 <= j < PAIRS and j % 2 == 1 else None
 
-        for J in range(LQ + 1):
-            stage_transpose(J)
-            if J < LQ:
-                stage_copy(J)
-                stage_quantise(J)
+        for J in range(QUANTISE_AHEAD):
+            transpose_job(J)
+            copy_out_job(J)
+            quantise_job(J)
+        spread_col_consts()
+        transpose_job(QUANTISE_AHEAD)
 
-        NS = 2 * NJ
-        s = 0
-        credit = 0.0
-        while s < NS or done[1] < len(items) or done[0] < len(pend):
-            if s < NS:
-                stage_mx(s)
-            if s + LQ + 1 < NS:
-                stage_transpose(s + LQ + 1)
-            if s + LQ < NS:
-                stage_copy(s + LQ)
-            odd = {}
-            for lag in range(LP3, LP3 + 6):
-                if 0 <= s - lag < NJ and (s - lag) % 2 == 1:
-                    odd[lag - LP3] = (s - lag) // 2
-            if s < NS:
-                stage_evacuate(s)
-            if s + LQ < NS:
-                stage_quantise(s + LQ)
-            if NJ <= s < NS:
-                stage_q(s)
-            if 0 <= s - LP3 < NJ:
-                stage_norm(s - LP3)
-            if 0 in odd:
-                stage_pow(odd[0])
-            if 2 in odd:
-                stage_tanh(odd[2])
-            if 3 in odd:
-                stage_factor(odd[3])
-            if 4 in odd:
-                stage_scale(odd[4], 0)
-            if 5 in odd:
-                stage_scale(odd[5], 1)
-            k = (s - NJ - 2) // 2
-            if (s - NJ) % 2 == 0 and k in VARB:
-                stage_pre(k)
-            if 18 <= s < 23:
-                stage_rowconst(0, s - 18)
-            if 30 <= s < 35:
-                stage_rowconst(1, s - 30)
-            follow(1)
-            credit = credit + (CD_CAP if s < NS else 100.0)
-            while done[1] < len(items):
-                kind, k, first_step = items[done[1]]
-                cost = 2.0 if kind == "sqrt" and k not in VARB else 1.0
-                if first_step > s or credit < cost:
+        step = 0
+        taken = 0
+        while step < JOBS or taken < len(scalar_passes):
+            if step < JOBS:
+                multiply_job(step)
+            if step + QUANTISE_AHEAD + 1 < JOBS:
+                transpose_job(step + QUANTISE_AHEAD + 1)
+            if step + QUANTISE_AHEAD < JOBS:
+                copy_out_job(step + QUANTISE_AHEAD)
+            if step < JOBS:
+                leave_psum_job(step)
+            if step + QUANTISE_AHEAD < JOBS:
+                quantise_job(step + QUANTISE_AHEAD)
+            if PAIRS <= step < JOBS:
+                q_job(step)
+
+            if 0 <= step - NORM_BEHIND < PAIRS:
+                norm_pair(step - NORM_BEHIND)
+            k = quad_completed(step, NORM_BEHIND)
+            if k is not None:
+                root_of_norm_quad(k)
+            k = quad_completed(step, TANH_BEHIND)
+            if k is not None:
+                tanh_quad(k)
+            k = quad_completed(step, FACTOR_BEHIND)
+            if k is not None:
+                factor_quad(k)
+            k = quad_completed(step, SCALE_BEHIND)
+            if k is not None:
+                scale_pair(2 * k)
+            k = quad_completed(step, SCALE_BEHIND + 1)
+            if k is not None:
+                scale_pair(2 * k + 1)
+                store_hyp_quad(k)
+            for half in range(2):
+                link = step - (PAIRS // 2) * (half + 1) - TANH_BEHIND
+                if 0 <= link < 5:
+                    row_constants(half, link)
+            k = quad_completed(step - PAIRS, 1)
+            if k in SECOND_FORM:
+                product_quad(k)
+
+            room = SCALAR_PASSES_A_STEP if step < JOBS else 2 * len(scalar_passes)
+            while taken < len(scalar_passes):
+                stage, follower, k = scalar_passes[taken]
+                passes = 2 if stage == roots_quad and k not in SECOND_FORM else 1
+                if passes > room or (stage == roots_quad and step < PAIRS + 2 * k + 1 + ROOTS_BEHIND):
                     break
-                done[1] += 1
-                credit -= cost
-                if kind == "sqrt":
-                    stage_sqrt(k)
-                else:
-                    if ("sqrt", k) in pend[done[0] :]:
-                        follow(0)
-                    stage_ln(k)
-                pend.append((kind, k))
-                if s >= NS:
-                    follow(1)
-            credit = min(credit, 2.0)
-            if s >= NS and done[1] == len(items):
-                follow(0)
-            s += 1
+                room -= passes
+                stage(k)
+                if taken > 0:
+                    scalar_passes[taken - 1][1](scalar_passes[taken - 1][2])
+                taken += 1
+            step += 1
+        scalar_passes[-1][1](scalar_passes[-1][2])

@@ -31,16 +31,16 @@ GAMMA_MIN = 1e-10
 
 QUANTISE_AHEAD = 2
 NORM_BEHIND = 2
-TANH_BEHIND = NORM_BEHIND + 2
-FACTOR_BEHIND = NORM_BEHIND + 3
-SCALE_BEHIND = NORM_BEHIND + 4
-ROOTS_BEHIND = 2
+TANH_BEHIND = NORM_BEHIND + 3
+FACTOR_BEHIND = NORM_BEHIND + 4
+SCALE_BEHIND = NORM_BEHIND + 6
+ROOTS_BEHIND = 3
 
 ROOT_LOG_RUNS = (9, 3)
 SECOND_FORM = (10, 11)
 SCALAR_PASSES_A_STEP = 2
 
-H_COPIES_ON_VECTOR = (5, 7, 9, 11, 13, 15)
+H_COPIES_ON_VECTOR = (5, 7, 9, 11, 13, 15, 17, 19)
 HYP_COPIES_ON_VECTOR = (33, 37, 41, 45)
 
 

import math
from contextlib import ExitStack

import concourse.mybir as mybir
from concourse.masks import make_identity

F32 = mybir.dt.float32
BF16 = mybir.dt.bfloat16
U32 = mybir.dt.uint32
U8 = mybir.dt.uint8
FP8X4 = mybir.dt.float8_e4m3fn_x4
ALU = mybir.AluOpType
ACT = mybir.ActivationFunctionType

B, H, D, N = 6144, 1024, 512, 256
FLOPS = 2 * B * H * D + 2 * B * D * N

P = 128
TILES = B // P
PAIRS = TILES // 2
QUADS = TILES // 4
JOBS = 2 * PAIRS
K_PASS = 4 * P

C = 3.0
SQRT_C = math.sqrt(C)
K_LOGIT = 1.0 / (0.07 * SQRT_C)
LOGIT_MIN = -K_LOGIT * math.log((2.0 - 1e-5) / 1e-5)
Z_MIN = SQRT_C * 1e-15
GAMMA_MIN = 1e-10

QUANTISE_AHEAD = 2
NORM_BEHIND = 2
TANH_BEHIND = NORM_BEHIND + 3
FACTOR_BEHIND = NORM_BEHIND + 4
SCALE_BEHIND = NORM_BEHIND + 6
ROOTS_BEHIND = 3

ROOT_LOG_RUNS = (9, 3)
SECOND_FORM = (10, 11)
SCALAR_PASSES_A_STEP = 2

H_COPIES_ON_VECTOR = (5, 7, 9, 11, 13, 15, 17, 19)
HYP_COPIES_ON_VECTOR = (33, 37, 41, 45)


def tile_hyperbolicuniform_pa_t_kernel(tc, h_mlp, W3, b3, prototypes, out_0, out_1):
    nc = tc.nc
    h_rows = h_mlp.rearrange("(p t) k -> p t k", t=TILES)
    hyp_rows = out_1.rearrange("(p t) d -> p t d", t=TILES)
    logit_rows = out_0.rearrange("(p t) j -> p t j", t=TILES)

    with ExitStack() as ctx:
        ctx.enter_context(tc.manual_schedule())
        const = ctx.enter_context(tc.tile_pool(name="const", bufs=1))
        h_pool = ctx.enter_context(tc.tile_pool(name="h_pool", bufs=4))
        row_pool = ctx.enter_context(tc.tile_pool(name="row_pool", bufs=QUADS))
        mx_pool = ctx.enter_context(tc.tile_pool(name="mx_pool", bufs=4))
        dist_pool = ctx.enter_context(tc.tile_pool(name="dist_pool", bufs=4))
        aux_pool = ctx.enter_context(tc.tile_pool(name="aux_pool", bufs=6))
        tr_psum = ctx.enter_context(tc.psum_pool(name="tr_psum", bufs=4))
        mm_psum = ctx.enter_context(tc.psum_pool(name="mm_psum", bufs=4))

        ident = const.tile([P, P], F32, name="ident")
        ident_bf = const.tile([P, P], BF16, name="ident_bf")
        bias_row = const.tile([P, D], BF16, name="bias_row")
        ones = const.tile([P, P], BF16, name="ones")
        minus_half = const.tile([P, 4], F32, name="minus_half")
        nc.gpsimd.memset(bias_row[:], 0.0)
        make_identity(nc, ident_bf[:])
        nc.gpsimd.memset(ones[:], 1.0)
        make_identity(nc, ident[:])
        nc.gpsimd.memset(minus_half[:], -0.5)

        proto = const.tile([P, 2, D], BF16, name="proto")
        nc.scalar.dma_start(out=proto[:], in_=prototypes.rearrange("(c p) d -> p c d", c=2))
        nc.scalar.dma_start(out=bias_row[0:1, :], in_=b3.unsqueeze(0))

        w_raw = const.tile([P, 2, 2, 2, D], BF16, name="w_raw")
        w_grouped = const.tile([P, 2, D, 4], BF16, name="w_grouped", align_bytes=64)
        w_codes = const.tile([P, 2, D], U32, name="w_codes", align_bytes=64)
        w_scales = const.tile([P, 2, D], U8, name="w_scales", align_bytes=64)
        for g in range(2):
            nc.sync.dma_start(
                out=w_raw[:, g],
                in_=W3[K_PASS * g : K_PASS * (g + 1), :].rearrange("(u p e) d -> p u e d", u=2, e=2),
            )

        h_quads = {}

        def load_h(k, pieces):
            h_quads[k] = h_pool.tile([P, 4, H], BF16, name="h_quad", tag="h_quad")
            n = 4 // pieces
            for a in range(0, 4, n):
                nc.sync.dma_start(out=h_quads[k][:, a : a + n, :], in_=h_rows[:, 4 * k + a : 4 * k + a + n, :])

        load_h(0, 2)
        load_h(1, 2)
        load_h(2, 1)
        load_h(3, 1)

        def regroup_w(g):
            nc.vector.tensor_copy(
                out=w_grouped[:, g].rearrange("p (c i) t -> p c t i", i=4),
                in_=w_raw[:, g].rearrange("p u e (c i) -> p c (u e) i", i=4),
            )

        def quantise_w(g):
            nc.vector.quantize_mx(
                out=w_codes[:, g, :].bitcast(FP8X4),
                scales=w_scales[:, g, :],
                in_=w_grouped[:, g].rearrange("p d t -> p (d t)"),
            )

        zz = const.tile([P, TILES], F32, name="zz")
        tanh_z = const.tile([P, TILES], F32, name="tanh_z")
        zz_floor = const.tile([P, TILES], F32, name="zz_floor")
        z_inv = const.tile([P, TILES], F32, name="z_inv")
        z = const.tile([P, TILES], F32, name="z")
        factor = const.tile([P, TILES], F32, name="factor")
        c_bn = const.tile([P, TILES], F32, name="c_bn")
        half_bn = const.tile([P, TILES], F32, name="half_bn")
        gamma = const.tile([P, TILES], F32, name="gamma")
        gamma_floor = const.tile([P, TILES], F32, name="gamma_floor")
        gamma_inv = const.tile([P, TILES], F32, name="gamma_inv")
        row_scale = const.tile([P, TILES], F32, name="row_scale")

        a_col = const.tile([P, 2], F32, name="a_col")
        beta_col = const.tile([P, 2], F32, name="beta_col")
        col_consts = const.tile([P, 4], F32, name="col_consts")
        proto_grouped = const.tile([P, N, 4], BF16, name="proto_grouped", align_bytes=64)
        proto_codes = const.tile([P, N], U32, name="proto_codes", align_bytes=64)
        proto_scales = const.tile([P, N], U8, name="proto_scales", align_bytes=64)
        col_bc = const.tile([P, 2, N], F32, name="col_bc")
        bias_bc = const.tile([P, D], F32, name="bias_bc")
        proto_squares = const.tile([P, D], BF16, name="proto_squares")

        for c in range(2):
            nc.scalar.activation(
                out=proto_squares[:], in_=proto[:, c, :], func=ACT.Square, accum_out=a_col[:, c : c + 1]
            )
        proto_t = []
        for c in range(2):
            proto_t.append(mm_psum.tile([P, 4, P], BF16, name="proto_t", tag="mm"))
            for t in range(4):
                nc.tensor.transpose(proto_t[c][:, t, :], proto[:, c, P * t : P * (t + 1)], ident_bf[:])
        bias_ps = mm_psum.tile([P, D], F32, name="bias_ps", tag="mm")
        nc.tensor.matmul(out=bias_ps[:], lhsT=ones[:], rhs=bias_row[:], start=True, stop=True)
        regroup_w(0)
        nc.vector.tensor_scalar(out=col_consts[:, 0:2], in0=a_col[:], scalar1=0.5, scalar2=None, op0=ALU.mult)
        nc.vector.tensor_scalar(out=beta_col[:], in0=a_col[:], scalar1=-C, scalar2=1.0, op0=ALU.mult, op1=ALU.add)
        regroup_w(1)
        nc.vector.reciprocal(out=col_consts[:, 2:4], in_=beta_col[:])
        quantise_w(0)
        for c in range(2):
            nc.scalar.copy(
                out=proto_grouped[:, P * c : P * (c + 1), :], in_=proto_t[c][:].rearrange("p t j -> p j t")
            )
        nc.scalar.copy(out=bias_bc[:], in_=bias_ps[:])
        quantise_w(1)
        nc.vector.quantize_mx(
            out=proto_codes[:].bitcast(FP8X4), scales=proto_scales[:], in_=proto_grouped[:].rearrange("p j t -> p (j t)")
        )

        def spread_col_consts():
            col_ps = mm_psum.tile([P, 4, P], F32, name="col_ps", tag="mm")
            for m in range(4):
                nc.tensor.matmul(
                    out=col_ps[:, m, :], lhsT=col_consts[:, m : m + 1].to_broadcast([P, P]), rhs=ident[:],
                    start=True, stop=True,
                )
            nc.scalar.copy(out=col_bc[:].rearrange("p v j -> p (v j)"), in_=col_ps[:].rearrange("p m j -> p (m j)"))

        row_quads = {}
        q_quads = {}
        transposed = {}
        grouped = {}
        codes = {}
        products = {}
        diffs = {}
        aux = {}

        def row_tile(t):
            return row_quads[t // 4][:, t % 4, :]

        def transpose_job(J):
            for i in range(2):
                t = 2 * J + i
                transposed[t] = tr_psum.tile([P, 4, P], F32, name="transposed", tag="tr")
                if J < PAIRS:
                    src = h_quads[t // 4][:].bitcast(F32)[:, t % 4, :]
                else:
                    src = row_tile(t - TILES)
                for c in range(4):
                    nc.tensor.transpose(transposed[t][:, c, :], src[:, P * c : P * (c + 1)], ident[:])
            if J < PAIRS and J % 2 == 1 and J // 2 + 4 < QUADS:
                load_h(J // 2 + 4, 1)

        def copy_out_job(J):
            if J < PAIRS:
                grouped[J] = mx_pool.tile([P, 2, 2, P, 4], BF16, name="h_grouped", tag="grouped", align_bytes=64)
                for i in range(2):
                    t = 2 * J + i
                    dst = grouped[J][:].bitcast(F32)[:, i]
                    src = transposed[t][:].rearrange("p (g u) b -> p g b u", u=2)
                    if t in H_COPIES_ON_VECTOR:
                        nc.vector.tensor_copy(out=dst, in_=src)
                    else:
                        nc.scalar.copy(out=dst, in_=src)
            else:
                grouped[J] = mx_pool.tile([P, 2, P, 4], BF16, name="hyp_grouped", tag="grouped", align_bytes=64)
                for i in range(2):
                    t = 2 * J + i
                    src = transposed[t][:].rearrange("p t b -> p b t")
                    if t - TILES in HYP_COPIES_ON_VECTOR:
                        nc.vector.tensor_copy(out=grouped[J][:, i], in_=src)
                    else:
                        nc.scalar.copy(out=grouped[J][:, i], in_=src)

        def quantise_job(J):
            words = 4 * P if J < PAIRS else 2 * P
            codes[J] = (
                mx_pool.tile([P, words], U32, name="codes", tag="codes", align_bytes=64),
                mx_pool.tile([P, words], U8, name="scales", tag="scales", align_bytes=64),
            )
            if J < PAIRS:
                flat = grouped[J][:].rearrange("p i g b t -> p (i g b t)")
            else:
                flat = grouped[J][:].rearrange("p i b t -> p (i b t)")
            nc.vector.quantize_mx(out=codes[J][0][:].bitcast(FP8X4), scales=codes[J][1][:], in_=flat)

        def multiply_job(J):
            words, scales = codes[J]
            if J < PAIRS:
                for i in range(2):
                    products[2 * J + i] = mm_psum.tile([P, D], F32, name="u_ps", tag="mm")
                    for g in range(2):
                        cols = slice(P * (2 * i + g), P * (2 * i + g + 1))
                        nc.tensor.matmul_mx(
                            out=products[2 * J + i][:],
                            lhsT=words[:, cols].bitcast(FP8X4),
                            lhsT_scale=scales[:, cols],
                            rhs=w_codes[:, g, :].bitcast(FP8X4),
                            rhs_scale=w_scales[:, g, :],
                            start=(g == 0),
                            stop=(g == 1),
                        )
            else:
                products[2 * J] = mm_psum.tile([P, 2, N], F32, name="x_ps", tag="mm")
                for i in range(2):
                    cols = slice(P * i, P * (i + 1))
                    nc.tensor.matmul_mx(
                        out=products[2 * J][:, i, :],
                        lhsT=words[:, cols].bitcast(FP8X4),
                        lhsT_scale=scales[:, cols],
                        rhs=proto_codes[:].bitcast(FP8X4),
                        rhs_scale=proto_scales[:],
                        start=True,
                        stop=True,
                    )

        def leave_psum_job(J):
            for i in range(2):
                if J < PAIRS:
                    t = 2 * J + i
                    if t % 4 == 0:
                        row_quads[t // 4] = row_pool.tile([P, 4, D], F32, name="row_quad", tag="quad")
                    nc.vector.tensor_tensor(out=row_tile(t), in0=products[t][:], in1=bias_bc[:], op=ALU.add)
                else:
                    t = 2 * J + i - TILES
                    diffs[t] = dist_pool.tile([P, N], F32, name="diff", tag="diff")
                    nc.vector.scalar_tensor_tensor(
                        out=diffs[t][:], in0=products[2 * J][:, i, :], scalar=half_bn[:, t : t + 1], in1=col_bc[:, 0, :],
                        op0=ALU.subtract, op1=ALU.subtract,
                    )

        def q_job(J):
            for t in (2 * J - TILES, 2 * J - TILES + 1):
                if t % 4 == 0:
                    q_quads[t // 4] = row_pool.tile([P, 4, N], F32, name="q_quad", tag="quad")
                nc.vector.scalar_tensor_tensor(
                    out=q_quads[t // 4][:, t % 4, :], in0=diffs[t][:], scalar=row_scale[:, t : t + 1], in1=col_bc[:, 1, :],
                    op0=ALU.mult, op1=ALU.mult,
                )

        def quad_cols(k):
            return slice(4 * k, 4 * k + 4)

        def norm_pair(j):
            for t in (2 * j, 2 * j + 1):
                scratch = dist_pool.tile([P, D], BF16, name="scratch", tag="scratch")
                nc.scalar.activation(
                    out=scratch[:], in_=row_tile(t), func=ACT.Square, scale=SQRT_C, accum_out=zz[:, t : t + 1]
                )

        def root_of_norm_quad(k):
            cols = quad_cols(k)
            nc.gpsimd.tensor_scalar(out=zz_floor[:, cols], in0=zz[:, cols], scalar1=Z_MIN * Z_MIN, scalar2=None, op0=ALU.max)
            nc.gpsimd.tensor_tensor(out=z_inv[:, cols], in0=zz_floor[:, cols], in1=minus_half[:], op=ALU.pow)
            nc.gpsimd.tensor_tensor(out=z[:, cols], in0=zz[:, cols], in1=z_inv[:, cols], op=ALU.mult)

        def tanh_quad(k):
            nc.scalar.activation(out=tanh_z[:, quad_cols(k)], in_=z[:, quad_cols(k)], func=ACT.Tanh)

        def factor_quad(k):
            cols = quad_cols(k)
            nc.gpsimd.tensor_tensor(out=factor[:, cols], in0=tanh_z[:, cols], in1=z_inv[:, cols], op=ALU.mult)

        def scale_pair(j):
            for t in (2 * j, 2 * j + 1):
                nc.vector.tensor_scalar(
                    out=row_tile(t), in0=row_tile(t), scalar1=factor[:, t : t + 1], scalar2=None, op0=ALU.mult
                )

        def store_hyp_quad(k):
            nc.sync.dma_start(out=hyp_rows[:, 4 * k : 4 * k + 4, :], in_=row_quads[k][:])

        def row_constants(half, link):
            cols = slice(PAIRS * half, PAIRS * (half + 1))
            if link == 0:
                nc.vector.tensor_tensor(out=c_bn[:, cols], in0=tanh_z[:, cols], in1=tanh_z[:, cols], op=ALU.mult)
            elif link == 1:
                nc.vector.tensor_scalar(
                    out=gamma[:, cols], in0=c_bn[:, cols], scalar1=-1.0, scalar2=1.0, op0=ALU.mult, op1=ALU.add
                )
                nc.vector.tensor_scalar(
                    out=half_bn[:, cols], in0=c_bn[:, cols], scalar1=0.5 / C, scalar2=None, op0=ALU.mult
                )
            elif link == 2:
                nc.vector.tensor_scalar(
                    out=gamma_floor[:, cols], in0=gamma[:, cols], scalar1=GAMMA_MIN, scalar2=None, op0=ALU.max
                )
            elif link == 3:
                nc.vector.reciprocal(out=gamma_inv[:, cols], in_=gamma_floor[:, cols])
            else:
                nc.vector.tensor_scalar(
                    out=row_scale[:, cols], in0=gamma_inv[:, cols], scalar1=-2.0 * C, scalar2=None, op0=ALU.mult
                )

        def flat_q(k, first=0, tiles=4):
            return q_quads[k][:, first : first + tiles, :].rearrange("p i j -> p (i j)")

        def product_quad(k):
            aux[k] = aux_pool.tile([P, 4 * N], F32, name="aux", tag="aux")
            nc.vector.scalar_tensor_tensor(
                out=aux[k][:], in0=flat_q(k), scalar=1.0, in1=flat_q(k), op0=ALU.add, op1=ALU.mult
            )

        def roots_quad(k):
            if k in SECOND_FORM:
                nc.scalar.activation(out=aux[k][:], in_=aux[k][:], func=ACT.Sqrt)
            else:
                aux[k] = aux_pool.tile([P, 4 * N], F32, name="aux", tag="aux")
                nc.scalar.activation(out=aux[k][:], in_=flat_q(k), func=ACT.Sqrt, bias=1.0)
                nc.scalar.activation(out=flat_q(k), in_=flat_q(k), func=ACT.Sqrt)

        def sum_quad(k):
            root, other = (aux[k][:], flat_q(k)) if k in SECOND_FORM else (flat_q(k), aux[k][:])
            nc.vector.scalar_tensor_tensor(out=flat_q(k), in0=root, scalar=0.0, in1=other, op0=ALU.max, op1=ALU.add)

        def leaving_pieces(k):
            return ((0, 2), (2, 2)) if k == QUADS - 1 else ((0, 4),)

        def log_quad(k):
            for first, tiles in leaving_pieces(k):
                piece = flat_q(k, first, tiles)
                if k in SECOND_FORM:
                    nc.scalar.activation(out=piece, in_=piece, func=ACT.Ln, scale=2.0, bias=1.0)
                else:
                    nc.scalar.activation(out=piece, in_=piece, func=ACT.Ln)

        def finish_quad(k):
            for first, tiles in leaving_pieces(k):
                piece = flat_q(k, first, tiles)
                nc.vector.tensor_scalar(
                    out=piece, in0=piece, scalar1=(-K_LOGIT if k in SECOND_FORM else -2.0 * K_LOGIT), scalar2=LOGIT_MIN,
                    op0=ALU.mult, op1=ALU.max,
                )
                nc.sync.dma_start(
                    out=logit_rows[:, 4 * k + first : 4 * k + first + tiles, :],
                    in_=q_quads[k][:, first : first + tiles, :],
                )

        scalar_passes = []
        first_quad = 0
        for run in ROOT_LOG_RUNS:
            quads = range(first_quad, first_quad + run)
            scalar_passes.extend([(roots_quad, sum_quad, k) for k in quads])
            scalar_passes.extend([(log_quad, finish_quad, k) for k in quads])
            first_quad += run

        def quad_completed(step, behind):
            j = step - behind
            return j // 2 if 0 <= j < PAIRS and j % 2 == 1 else None

        for J in range(QUANTISE_AHEAD):
            transpose_job(J)
            copy_out_job(J)
            quantise_job(J)
        spread_col_consts()
        transpose_job(QUANTISE_AHEAD)

        step = 0
        taken = 0
        while step < JOBS or taken < len(scalar_passes):
            if step < JOBS:
                multiply_job(step)
            if step + QUANTISE_AHEAD + 1 < JOBS:
                transpose_job(step + QUANTISE_AHEAD + 1)
            if step + QUANTISE_AHEAD < JOBS:
                copy_out_job(step + QUANTISE_AHEAD)
            if step < JOBS:
                leave_psum_job(step)
            if step + QUANTISE_AHEAD < JOBS:
                quantise_job(step + QUANTISE_AHEAD)
            if PAIRS <= step < JOBS:
                q_job(step)

            if 0 <= step - NORM_BEHIND < PAIRS:
                norm_pair(step - NORM_BEHIND)
            k = quad_completed(step, NORM_BEHIND)
            if k is not None:
                root_of_norm_quad(k)
            k = quad_completed(step, TANH_BEHIND)
            if k is not None:
                tanh_quad(k)
            k = quad_completed(step, FACTOR_BEHIND)
            if k is not None:
                factor_quad(k)
            k = quad_completed(step, SCALE_BEHIND)
            if k is not None:
                scale_pair(2 * k)
            k = quad_completed(step, SCALE_BEHIND + 1)
            if k is not None:
                scale_pair(2 * k + 1)
                store_hyp_quad(k)
            for half in range(2):
                link = step - (PAIRS // 2) * (half + 1) - TANH_BEHIND
                if 0 <= link < 5:
                    row_constants(half, link)
            k = quad_completed(step - PAIRS, 1)
            if k in SECOND_FORM:
                product_quad(k)

            room = SCALAR_PASSES_A_STEP if step < JOBS else 2 * len(scalar_passes)
            while taken < len(scalar_passes):
                stage, follower, k = scalar_passes[taken]
                passes = 2 if stage == roots_quad and k not in SECOND_FORM else 1
                if passes > room or (stage == roots_quad and step < PAIRS + 2 * k + 1 + ROOTS_BEHIND):
                    break
                room -= passes
                stage(k)
                if taken > 0:
                    scalar_passes[taken - 1][1](scalar_passes[taken - 1][2])
                taken += 1
            step += 1
        scalar_passes[-1][1](scalar_passes[-1][2])
